import numpy as np
import ml_dtypes

BF16 = ml_dtypes.bfloat16


def bf(x):
    return np.asarray(x, np.float32).astype(BF16)


def f32(x):
    return np.asarray(x, np.float32)


def f64(x):
    return np.asarray(x).astype(np.float64)


def striped(idx):
    return np.tile(idx.reshape(-1, 16).T, (8, 1))


C, S, N, GS, NC, H, K = 384, 2048, 4096, 32, 128, 1024, 4
EPS, LIM, TERMS = 1e-5, 6.0, 150


def erf(a):
    a = np.asarray(a, np.float64)
    b = np.clip(a, -LIM, LIM)
    term = b.copy()
    tot = b.copy()
    for n in range(1, TERMS):
        term = term * 2.0 * b * b / (2.0 * n + 1.0)
        tot = tot + term
    r = 2.0 / np.sqrt(np.pi) * np.exp(-b * b) * tot
    return np.where(np.abs(a) > LIM, np.sign(a), r)


def gelu(v):
    return 0.5 * v * (1.0 + erf(v / np.sqrt(2.0)))


def setup_inputs():
    idx = np.concatenate([np.random.permutation(S)[:H] for _ in range(K)])
    return {"x": f32(np.random.standard_normal((C, S))), "attn": f32(0.5 * np.random.standard_normal((C, N))), "bn_mean": f32(2.0 + 0.3 * np.random.standard_normal((C, 1))), "bn_var": f32(0.2 + 0.2 * np.random.random_sample((C, 1))), "bn_g": f32(1.0 + 0.1 * np.random.standard_normal((C, 1))), "bn_b": f32(0.1 * np.random.standard_normal((C, 1))), "offs": striped(idx)}


def reference(x, attn, bn_mean, bn_var, bn_g, bn_b, offs):
    idx = offs[:16].T.reshape(-1)
    y = f64(x)[:, idx] + f64(attn)
    y = y.reshape(C, NC, GS)
    pool = y.max(axis=-1) + y.mean(axis=-1)
    z = (pool - f64(bn_mean)) / np.sqrt(f64(bn_var) + EPS) * f64(bn_g) + f64(bn_b)
    return gelu(z)

@@ -1,0 +1,96 @@
+import concourse.mybir as mybir
+from concourse.masks import make_identity
+
+F32 = mybir.dt.float32
+U16 = mybir.dt.uint16
+ALU = mybir.AluOpType
+ACT = mybir.ActivationFunctionType
+AXIS_X = mybir.AxisListType.X
+
+P = 128
+CHANNELS = 384
+BLOCKS = CHANNELS // P
+STORE = 2048
+ENTRIES = 4096
+GROUP = 32
+CENTRES = ENTRIES // GROUP
+PIECE = 1024
+PIECES = ENTRIES // PIECE
+PER_COLUMN = 16
+EPS = 1e-5
+PARAMS = 4
+
+
+def tile_block_kernel(tc, x, attn, bn_mean, bn_var, bn_g, bn_b, offs, out):
+    nc = tc.nc
+    with (
+        tc.tile_pool(name="held", bufs=1) as held,
+        tc.tile_pool(name="work", bufs=2) as work,
+        tc.psum_pool(name="psum", bufs=1) as psum,
+    ):
+        offsets = held.tile([P, ENTRIES // PER_COLUMN], U16, name="offsets")
+        nc.sync.dma_start(offsets[:], offs)
+
+        rows = held.tile([PARAMS, CHANNELS], F32, name="rows")
+        for i, vector in enumerate((bn_mean, bn_var, bn_g, bn_b)):
+            nc.scalar.dma_start(rows[i : i + 1, :], vector.rearrange("c o -> o c"))
+
+        stores = []
+        branches = []
+        for b in range(BLOCKS):
+            channels = slice(b * P, (b + 1) * P)
+            store = held.tile([P, STORE], F32, name=f"store{b}")
+            nc.sync.dma_start(store[:], x[channels, :])
+            branch = held.tile([P, ENTRIES], F32, name=f"branch{b}")
+            for k in range(PIECES):
+                entries = slice(k * PIECE, (k + 1) * PIECE)
+                nc.sync.dma_start(branch[:, entries], attn[channels, entries])
+            stores.append(store)
+            branches.append(branch)
+
+        identity = held.tile([P, P], F32, name="identity")
+        make_identity(nc, identity[:])
+        columns_psum = psum.tile([P, BLOCKS * PARAMS], F32, name="columns_psum")
+        for b in range(BLOCKS):
+            nc.tensor.matmul(
+                columns_psum[:, b * PARAMS : (b + 1) * PARAMS],
+                rows[:, b * P : (b + 1) * P],
+                identity[:PARAMS, :PARAMS],
+                start=True,
+                stop=True,
+            )
+        columns = held.tile([P, BLOCKS, PARAMS], F32, name="columns")
+        nc.vector.tensor_copy(columns[:].rearrange("p b i -> p (b i)"), columns_psum[:])
+        mean, var, gain, shift = (columns[:, :, i] for i in range(PARAMS))
+
+        scale = held.tile([P, BLOCKS], F32, name="scale")
+        bias = held.tile([P, BLOCKS], F32, name="bias")
+        nc.vector.tensor_scalar_add(scale[:], var, EPS)
+        nc.scalar.sqrt(scale[:], scale[:])
+        nc.vector.reciprocal(scale[:], scale[:])
+        nc.vector.tensor_mul(scale[:], scale[:], gain)
+        nc.vector.tensor_mul(bias[:], mean, scale[:])
+        nc.vector.tensor_sub(bias[:], shift, bias[:])
+
+        for b in range(BLOCKS):
+            summed = work.tile([P, ENTRIES], F32, name="summed")
+            for k in range(PIECES):
+                entries = slice(k * PIECE, (k + 1) * PIECE)
+                piece = offsets[:, k * PIECE // PER_COLUMN : (k + 1) * PIECE // PER_COLUMN]
+                nc.vector.tensor_tensor(
+                    summed[:, entries], stores[b][:].indirect(piece), branches[b][:, entries], ALU.add
+                )
+
+            groups = summed[:].rearrange("p (t r) -> p t r", r=GROUP)
+            largest = work.tile([P, CENTRES], F32, name="largest")
+            total = work.tile([P, CENTRES], F32, name="total")
+            nc.vector.tensor_reduce(largest[:], groups, AXIS_X, ALU.max)
+            nc.vector.tensor_reduce(total[:], groups, AXIS_X, ALU.add)
+
+            pooled = work.tile([P, CENTRES], F32, name="pooled")
+            nc.vector.scalar_tensor_tensor(pooled[:], total[:], 1.0 / GROUP, largest[:], ALU.mult, ALU.add)
+            result = work.tile([P, CENTRES], F32, name="result")
+            nc.scalar.activation(
+                result[:], pooled[:], ACT.Gelu, bias=bias[:, b : b + 1], scale=scale[:, b : b + 1]
+            )
+            nc.sync.dma_start(out[b * P : (b + 1) * P, :], result[:])

@@ -19,6 +19,10 @@ PIECES = ENTRIES // PIECE
 PER_COLUMN = 16
 EPS = 1e-5
 PARAMS = 4
+LANES = 4
+STEPS = GROUP // LANES
+PIECE_CENTRES = PIECE // GROUP
+FLOPS = 3 * CHANNELS * ENTRIES
 
 
 def tile_block_kernel(tc, x, attn, bn_mean, bn_var, bn_g, bn_b, offs, out):
@@ -27,6 +31,7 @@ def tile_block_kernel(tc, x, attn, bn_mean, bn_var, bn_g, bn_b, offs, out):
         tc.tile_pool(name="held", bufs=1) as held,
         tc.tile_pool(name="work", bufs=2) as work,
         tc.psum_pool(name="psum", bufs=1) as psum,
+        tc.psum_pool(name="means", bufs=2) as means,
     ):
         offsets = held.tile([P, ENTRIES // PER_COLUMN], U16, name="offsets")
         nc.sync.dma_start(offsets[:], offs)
@@ -50,6 +55,8 @@ def tile_block_kernel(tc, x, attn, bn_mean, bn_var, bn_g, bn_b, offs, out):
 
         identity = held.tile([P, P], F32, name="identity")
         make_identity(nc, identity[:])
+        averager = held.tile([P, P], F32, name="averager")
+        nc.scalar.mul(averager[:], identity[:], 1.0 / GROUP)
         columns_psum = psum.tile([P, BLOCKS * PARAMS], F32, name="columns_psum")
         for b in range(BLOCKS):
             nc.tensor.matmul(
@@ -74,21 +81,27 @@ def tile_block_kernel(tc, x, attn, bn_mean, bn_var, bn_g, bn_b, offs, out):
 
         for b in range(BLOCKS):
             summed = work.tile([P, ENTRIES], F32, name="summed")
+            partial = means.tile([P, CENTRES, LANES], F32, name="partial")
             for k in range(PIECES):
                 entries = slice(k * PIECE, (k + 1) * PIECE)
                 piece = offsets[:, k * PIECE // PER_COLUMN : (k + 1) * PIECE // PER_COLUMN]
                 nc.vector.tensor_tensor(
                     summed[:, entries], stores[b][:].indirect(piece), branches[b][:, entries], ALU.add
                 )
+                runs = summed[:, entries].rearrange("p (t s l) -> p s t l", s=STEPS, l=LANES)
+                centres = slice(k * PIECE_CENTRES, (k + 1) * PIECE_CENTRES)
+                for s in range(STEPS):
+                    nc.tensor.matmul(
+                        partial[:, centres, :], averager[:], runs[:, s], start=(s == 0), stop=(s == STEPS - 1)
+                    )
 
-            groups = summed[:].rearrange("p (t r) -> p t r", r=GROUP)
             largest = work.tile([P, CENTRES], F32, name="largest")
-            total = work.tile([P, CENTRES], F32, name="total")
-            nc.vector.tensor_reduce(largest[:], groups, AXIS_X, ALU.max)
-            nc.vector.tensor_reduce(total[:], groups, AXIS_X, ALU.add)
+            average = work.tile([P, CENTRES], F32, name="average")
+            nc.vector.tensor_reduce(largest[:], summed[:].rearrange("p (t r) -> p t r", r=GROUP), AXIS_X, ALU.max)
+            nc.vector.tensor_reduce(average[:], partial[:], AXIS_X, ALU.add)
 
             pooled = work.tile([P, CENTRES], F32, name="pooled")
-            nc.vector.scalar_tensor_tensor(pooled[:], total[:], 1.0 / GROUP, largest[:], ALU.mult, ALU.add)
+            nc.vector.tensor_add(pooled[:], largest[:], average[:])
             result = work.tile([P, CENTRES], F32, name="result")
             nc.scalar.activation(
                 result[:], pooled[:], ACT.Gelu, bias=bias[:, b : b + 1], scale=scale[:, b : b + 1]

@@ -19,9 +19,10 @@ PIECES = ENTRIES // PIECE
 PER_COLUMN = 16
 EPS = 1e-5
 PARAMS = 4
-LANES = 4
+HALF = ENTRIES // 2
+HALF_CENTRES = HALF // GROUP
+LANES = 2
 STEPS = GROUP // LANES
-PIECE_CENTRES = PIECE // GROUP
 FLOPS = 3 * CHANNELS * ENTRIES
 
 
@@ -29,9 +30,9 @@ def tile_block_kernel(tc, x, attn, bn_mean, bn_var, bn_g, bn_b, offs, out):
     nc = tc.nc
     with (
         tc.tile_pool(name="held", bufs=1) as held,
-        tc.tile_pool(name="work", bufs=2) as work,
+        tc.tile_pool(name="work", bufs=BLOCKS) as work,
         tc.psum_pool(name="psum", bufs=1) as psum,
-        tc.psum_pool(name="means", bufs=2) as means,
+        tc.psum_pool(name="sums", bufs=BLOCKS) as sums,
     ):
         offsets = held.tile([P, ENTRIES // PER_COLUMN], U16, name="offsets")
         nc.sync.dma_start(offsets[:], offs)
@@ -81,27 +82,26 @@ def tile_block_kernel(tc, x, attn, bn_mean, bn_var, bn_g, bn_b, offs, out):
 
         for b in range(BLOCKS):
             summed = work.tile([P, ENTRIES], F32, name="summed")
-            partial = means.tile([P, CENTRES, LANES], F32, name="partial")
-            for k in range(PIECES):
-                entries = slice(k * PIECE, (k + 1) * PIECE)
-                piece = offsets[:, k * PIECE // PER_COLUMN : (k + 1) * PIECE // PER_COLUMN]
-                nc.vector.tensor_tensor(
-                    summed[:, entries], stores[b][:].indirect(piece), branches[b][:, entries], ALU.add
-                )
-                runs = summed[:, entries].rearrange("p (t s l) -> p s t l", s=STEPS, l=LANES)
-                centres = slice(k * PIECE_CENTRES, (k + 1) * PIECE_CENTRES)
+            partial = sums.tile([P, CENTRES, LANES], F32, name="partial")
+            for h in range(ENTRIES // HALF):
+                for k in range(h * HALF // PIECE, (h + 1) * HALF // PIECE):
+                    entries = slice(k * PIECE, (k + 1) * PIECE)
+                    piece = offsets[:, k * PIECE // PER_COLUMN : (k + 1) * PIECE // PER_COLUMN]
+                    nc.vector.tensor_tensor(
+                        summed[:, entries], stores[b][:].indirect(piece), branches[b][:, entries], ALU.add
+                    )
+                runs = summed[:, h * HALF : (h + 1) * HALF].rearrange("p (t s l) -> p s t l", s=STEPS, l=LANES)
+                centres = slice(h * HALF_CENTRES, (h + 1) * HALF_CENTRES)
                 for s in range(STEPS):
                     nc.tensor.matmul(
                         partial[:, centres, :], averager[:], runs[:, s], start=(s == 0), stop=(s == STEPS - 1)
                     )
 
             largest = work.tile([P, CENTRES], F32, name="largest")
-            average = work.tile([P, CENTRES], F32, name="average")
             nc.vector.tensor_reduce(largest[:], summed[:].rearrange("p (t r) -> p t r", r=GROUP), AXIS_X, ALU.max)
-            nc.vector.tensor_reduce(average[:], partial[:], AXIS_X, ALU.add)
-
             pooled = work.tile([P, CENTRES], F32, name="pooled")
-            nc.vector.tensor_add(pooled[:], largest[:], average[:])
+            nc.vector.tensor_add(pooled[:], partial[:, :, 0], largest[:])
+            nc.vector.tensor_add(pooled[:], partial[:, :, 1], pooled[:])
             result = work.tile([P, CENTRES], F32, name="result")
             nc.scalar.activation(
                 result[:], pooled[:], ACT.Gelu, bias=bias[:, b : b + 1], scale=scale[:, b : b + 1]

@@ -19,10 +19,9 @@ PIECES = ENTRIES // PIECE
 PER_COLUMN = 16
 EPS = 1e-5
 PARAMS = 4
-HALF = ENTRIES // 2
-HALF_CENTRES = HALF // GROUP
-LANES = 2
+LANES = 4
 STEPS = GROUP // LANES
+PIECE_CENTRES = PIECE // GROUP
 FLOPS = 3 * CHANNELS * ENTRIES
 
 
@@ -30,9 +29,9 @@ def tile_block_kernel(tc, x, attn, bn_mean, bn_var, bn_g, bn_b, offs, out):
     nc = tc.nc
     with (
         tc.tile_pool(name="held", bufs=1) as held,
-        tc.tile_pool(name="work", bufs=BLOCKS) as work,
+        tc.tile_pool(name="work", bufs=2) as work,
         tc.psum_pool(name="psum", bufs=1) as psum,
-        tc.psum_pool(name="sums", bufs=BLOCKS) as sums,
+        tc.psum_pool(name="sums", bufs=2) as sums,
     ):
         offsets = held.tile([P, ENTRIES // PER_COLUMN], U16, name="offsets")
         nc.sync.dma_start(offsets[:], offs)
@@ -80,30 +79,41 @@ def tile_block_kernel(tc, x, attn, bn_mean, bn_var, bn_g, bn_b, offs, out):
         nc.vector.tensor_mul(bias[:], mean, scale[:])
         nc.vector.tensor_sub(bias[:], shift, bias[:])
 
-        for b in range(BLOCKS):
-            summed = work.tile([P, ENTRIES], F32, name="summed")
-            partial = sums.tile([P, CENTRES, LANES], F32, name="partial")
-            for h in range(ENTRIES // HALF):
-                for k in range(h * HALF // PIECE, (h + 1) * HALF // PIECE):
+        summed_of = []
+        lanes_of = []
+        for b in range(BLOCKS + 1):
+            if b < BLOCKS:
+                summed = work.tile([P, ENTRIES], F32, name="summed")
+                partial = sums.tile([P, CENTRES, LANES], F32, name="partial")
+                for k in range(PIECES):
                     entries = slice(k * PIECE, (k + 1) * PIECE)
                     piece = offsets[:, k * PIECE // PER_COLUMN : (k + 1) * PIECE // PER_COLUMN]
                     nc.vector.tensor_tensor(
                         summed[:, entries], stores[b][:].indirect(piece), branches[b][:, entries], ALU.add
                     )
-                runs = summed[:, h * HALF : (h + 1) * HALF].rearrange("p (t s l) -> p s t l", s=STEPS, l=LANES)
-                centres = slice(h * HALF_CENTRES, (h + 1) * HALF_CENTRES)
-                for s in range(STEPS):
-                    nc.tensor.matmul(
-                        partial[:, centres, :], averager[:], runs[:, s], start=(s == 0), stop=(s == STEPS - 1)
-                    )
+                    runs = summed[:, entries].rearrange("p (t s l) -> p s t l", s=STEPS, l=LANES)
+                    centres = slice(k * PIECE_CENTRES, (k + 1) * PIECE_CENTRES)
+                    for s in range(STEPS):
+                        nc.tensor.matmul(
+                            partial[:, centres, :], averager[:], runs[:, s], start=(s == 0), stop=(s == STEPS - 1)
+                        )
+                lanes = work.tile([P, CENTRES, LANES], F32, name="lanes")
+                nc.scalar.copy(lanes[:], partial[:])
+                summed_of.append(summed)
+                lanes_of.append(lanes)
 
-            largest = work.tile([P, CENTRES], F32, name="largest")
-            nc.vector.tensor_reduce(largest[:], summed[:].rearrange("p (t r) -> p t r", r=GROUP), AXIS_X, ALU.max)
-            pooled = work.tile([P, CENTRES], F32, name="pooled")
-            nc.vector.tensor_add(pooled[:], partial[:, :, 0], largest[:])
-            nc.vector.tensor_add(pooled[:], partial[:, :, 1], pooled[:])
-            result = work.tile([P, CENTRES], F32, name="result")
-            nc.scalar.activation(
-                result[:], pooled[:], ACT.Gelu, bias=bias[:, b : b + 1], scale=scale[:, b : b + 1]
-            )
-            nc.sync.dma_start(out[b * P : (b + 1) * P, :], result[:])
+            if b >= 1:
+                done = b - 1
+                largest = work.tile([P, CENTRES], F32, name="largest")
+                nc.vector.tensor_reduce(
+                    largest[:], summed_of[done][:].rearrange("p (t r) -> p t r", r=GROUP), AXIS_X, ALU.max
+                )
+                pooled = sums.tile([P, CENTRES], F32, name="pooled")
+                for l in range(LANES):
+                    nc.tensor.matmul(pooled[:], identity[:], lanes_of[done][:, :, l], start=(l == 0), stop=False)
+                nc.tensor.matmul(pooled[:], identity[:], largest[:], start=False, stop=True)
+                result = work.tile([P, CENTRES], F32, name="result")
+                nc.scalar.activation(
+                    result[:], pooled[:], ACT.Gelu, bias=bias[:, done : done + 1], scale=scale[:, done : done + 1]
+                )
+                nc.sync.dma_start(out[done * P : (done + 1) * P, :], result[:])

@@ -12,16 +12,16 @@ CHANNELS = 384
 BLOCKS = CHANNELS // P
 STORE = 2048
 ENTRIES = 4096
+PER_COLUMN = 16
 GROUP = 32
 CENTRES = ENTRIES // GROUP
 PIECE = 1024
 PIECES = ENTRIES // PIECE
-PER_COLUMN = 16
-EPS = 1e-5
-PARAMS = 4
+PIECE_CENTRES = PIECE // GROUP
 LANES = 4
 STEPS = GROUP // LANES
-PIECE_CENTRES = PIECE // GROUP
+EPS = 1e-5
+PARAMS = 4
 FLOPS = 3 * CHANNELS * ENTRIES
 
 
@@ -29,9 +29,9 @@ def tile_block_kernel(tc, x, attn, bn_mean, bn_var, bn_g, bn_b, offs, out):
     nc = tc.nc
     with (
         tc.tile_pool(name="held", bufs=1) as held,
+        tc.psum_pool(name="held_psum", bufs=1) as held_psum,
         tc.tile_pool(name="work", bufs=2) as work,
-        tc.psum_pool(name="psum", bufs=1) as psum,
-        tc.psum_pool(name="sums", bufs=2) as sums,
+        tc.psum_pool(name="work_psum", bufs=2) as work_psum,
     ):
         offsets = held.tile([P, ENTRIES // PER_COLUMN], U16, name="offsets")
         nc.sync.dma_start(offsets[:], offs)
@@ -57,63 +57,50 @@ def tile_block_kernel(tc, x, attn, bn_mean, bn_var, bn_g, bn_b, offs, out):
         make_identity(nc, identity[:])
         averager = held.tile([P, P], F32, name="averager")
         nc.scalar.mul(averager[:], identity[:], 1.0 / GROUP)
-        columns_psum = psum.tile([P, BLOCKS * PARAMS], F32, name="columns_psum")
+
+        columns = held_psum.tile([P, BLOCKS, PARAMS], F32, name="columns")
         for b in range(BLOCKS):
             nc.tensor.matmul(
-                columns_psum[:, b * PARAMS : (b + 1) * PARAMS],
-                rows[:, b * P : (b + 1) * P],
-                identity[:PARAMS, :PARAMS],
-                start=True,
-                stop=True,
+                columns[:, b, :], rows[:, b * P : (b + 1) * P], identity[:PARAMS, :PARAMS], start=True, stop=True
             )
-        columns = held.tile([P, BLOCKS, PARAMS], F32, name="columns")
-        nc.vector.tensor_copy(columns[:].rearrange("p b i -> p (b i)"), columns_psum[:])
-        mean, var, gain, shift = (columns[:, :, i] for i in range(PARAMS))
+        running_mean, running_var, gain, shift = (columns[:, :, i] for i in range(PARAMS))
 
+        deviation = held.tile([P, BLOCKS], F32, name="deviation")
+        inverse = held.tile([P, BLOCKS], F32, name="inverse")
         scale = held.tile([P, BLOCKS], F32, name="scale")
+        scaled_mean = held.tile([P, BLOCKS], F32, name="scaled_mean")
         bias = held.tile([P, BLOCKS], F32, name="bias")
-        nc.vector.tensor_scalar_add(scale[:], var, EPS)
-        nc.scalar.sqrt(scale[:], scale[:])
-        nc.vector.reciprocal(scale[:], scale[:])
-        nc.vector.tensor_mul(scale[:], scale[:], gain)
-        nc.vector.tensor_mul(bias[:], mean, scale[:])
-        nc.vector.tensor_sub(bias[:], shift, bias[:])
+        nc.scalar.activation(deviation[:], running_var, ACT.Sqrt, bias=EPS)
+        nc.vector.reciprocal(inverse[:], deviation[:])
+        nc.vector.tensor_mul(scale[:], gain, inverse[:])
+        nc.vector.tensor_mul(scaled_mean[:], running_mean, scale[:])
+        nc.vector.tensor_sub(bias[:], shift, scaled_mean[:])
 
-        summed_of = []
-        lanes_of = []
-        for b in range(BLOCKS + 1):
-            if b < BLOCKS:
-                summed = work.tile([P, ENTRIES], F32, name="summed")
-                partial = sums.tile([P, CENTRES, LANES], F32, name="partial")
-                for k in range(PIECES):
-                    entries = slice(k * PIECE, (k + 1) * PIECE)
-                    piece = offsets[:, k * PIECE // PER_COLUMN : (k + 1) * PIECE // PER_COLUMN]
-                    nc.vector.tensor_tensor(
-                        summed[:, entries], stores[b][:].indirect(piece), branches[b][:, entries], ALU.add
+        for b in range(BLOCKS):
+            summed = work.tile([P, ENTRIES], F32, name="summed")
+            partial = work_psum.tile([P, CENTRES, LANES], F32, name="partial")
+            for k in range(PIECES):
+                entries = slice(k * PIECE, (k + 1) * PIECE)
+                piece = offsets[:, k * PIECE // PER_COLUMN : (k + 1) * PIECE // PER_COLUMN]
+                nc.vector.tensor_tensor(
+                    summed[:, entries], stores[b][:].indirect(piece), branches[b][:, entries], ALU.add
+                )
+                runs = summed[:, entries].rearrange("p (t s l) -> p s t l", s=STEPS, l=LANES)
+                centres = slice(k * PIECE_CENTRES, (k + 1) * PIECE_CENTRES)
+                for s in range(STEPS):
+                    nc.tensor.matmul(
+                        partial[:, centres, :], averager[:], runs[:, s], start=(s == 0), stop=(s == STEPS - 1)
                     )
-                    runs = summed[:, entries].rearrange("p (t s l) -> p s t l", s=STEPS, l=LANES)
-                    centres = slice(k * PIECE_CENTRES, (k + 1) * PIECE_CENTRES)
-                    for s in range(STEPS):
-                        nc.tensor.matmul(
-                            partial[:, centres, :], averager[:], runs[:, s], start=(s == 0), stop=(s == STEPS - 1)
-                        )
-                lanes = work.tile([P, CENTRES, LANES], F32, name="lanes")
-                nc.scalar.copy(lanes[:], partial[:])
-                summed_of.append(summed)
-                lanes_of.append(lanes)
 
-            if b >= 1:
-                done = b - 1
-                largest = work.tile([P, CENTRES], F32, name="largest")
-                nc.vector.tensor_reduce(
-                    largest[:], summed_of[done][:].rearrange("p (t r) -> p t r", r=GROUP), AXIS_X, ALU.max
-                )
-                pooled = sums.tile([P, CENTRES], F32, name="pooled")
-                for l in range(LANES):
-                    nc.tensor.matmul(pooled[:], identity[:], lanes_of[done][:, :, l], start=(l == 0), stop=False)
-                nc.tensor.matmul(pooled[:], identity[:], largest[:], start=False, stop=True)
-                result = work.tile([P, CENTRES], F32, name="result")
-                nc.scalar.activation(
-                    result[:], pooled[:], ACT.Gelu, bias=bias[:, done : done + 1], scale=scale[:, done : done + 1]
-                )
-                nc.sync.dma_start(out[done * P : (done + 1) * P, :], result[:])
+            largest = work.tile([P, CENTRES], F32, name="largest")
+            average = work.tile([P, CENTRES], F32, name="average")
+            pooled = work.tile([P, CENTRES], F32, name="pooled")
+            nc.vector.tensor_reduce(largest[:], summed[:].rearrange("p (t r) -> p t r", r=GROUP), AXIS_X, ALU.max)
+            nc.vector.tensor_reduce(average[:], partial[:], AXIS_X, ALU.add)
+            nc.vector.tensor_add(pooled[:], largest[:], average[:])
+
+            result = work.tile([P, CENTRES], F32, name="result")
+            nc.scalar.activation(
+                result[:], pooled[:], ACT.Gelu, bias=bias[:, b : b + 1], scale=scale[:, b : b + 1]
+            )
+            nc.sync.dma_start(out[b * P : (b + 1) * P, :], result[:])

@@ -15,9 +15,8 @@ ENTRIES = 4096
 PER_COLUMN = 16
 GROUP = 32
 CENTRES = ENTRIES // GROUP
-PIECE = 1024
-PIECES = ENTRIES // PIECE
-PIECE_CENTRES = PIECE // GROUP
+CUTS = (0, 1024, 2048, 3072, 4096)
+FIRST_CUTS = (0, 256) + CUTS[1:]
 LANES = 4
 STEPS = GROUP // LANES
 EPS = 1e-5
@@ -25,38 +24,44 @@ PARAMS = 4
 FLOPS = 3 * CHANNELS * ENTRIES
 
 
+def pieces_of(b):
+    cuts = FIRST_CUTS if b == 0 else CUTS
+    return list(zip(cuts[:-1], cuts[1:]))
+
+
 def tile_block_kernel(tc, x, attn, bn_mean, bn_var, bn_g, bn_b, offs, out):
     nc = tc.nc
     with (
         tc.tile_pool(name="held", bufs=1) as held,
         tc.psum_pool(name="held_psum", bufs=1) as held_psum,
-        tc.tile_pool(name="work", bufs=2) as work,
-        tc.psum_pool(name="work_psum", bufs=2) as work_psum,
+        tc.tile_pool(name="work", bufs=BLOCKS) as work,
+        tc.psum_pool(name="work_psum", bufs=BLOCKS) as work_psum,
     ):
         offsets = held.tile([P, ENTRIES // PER_COLUMN], U16, name="offsets")
         nc.sync.dma_start(offsets[:], offs)
 
-        rows = held.tile([PARAMS, CHANNELS], F32, name="rows")
-        for i, vector in enumerate((bn_mean, bn_var, bn_g, bn_b)):
-            nc.scalar.dma_start(rows[i : i + 1, :], vector.rearrange("c o -> o c"))
-
         stores = []
         branches = []
+        loads = []
         for b in range(BLOCKS):
             channels = slice(b * P, (b + 1) * P)
             store = held.tile([P, STORE], F32, name=f"store{b}")
-            nc.sync.dma_start(store[:], x[channels, :])
+            loads.append((store[:], x[channels, :]))
             branch = held.tile([P, ENTRIES], F32, name=f"branch{b}")
-            for k in range(PIECES):
-                entries = slice(k * PIECE, (k + 1) * PIECE)
-                nc.sync.dma_start(branch[:, entries], attn[channels, entries])
+            for first, end in pieces_of(b):
+                loads.append((branch[:, first:end], attn[channels, first:end]))
             stores.append(store)
             branches.append(branch)
+        for n, (part, source) in enumerate(loads):
+            queue = nc.sync if n % 2 == 0 else nc.scalar
+            queue.dma_start(part, source)
+
+        rows = held.tile([PARAMS, CHANNELS], F32, name="rows")
+        for i, vector in enumerate((bn_mean, bn_var, bn_g, bn_b)):
+            nc.sync.dma_start(rows[i : i + 1, :], vector.rearrange("c o -> o c"))
 
         identity = held.tile([P, P], F32, name="identity")
         make_identity(nc, identity[:])
-        averager = held.tile([P, P], F32, name="averager")
-        nc.scalar.mul(averager[:], identity[:], 1.0 / GROUP)
 
         columns = held_psum.tile([P, BLOCKS, PARAMS], F32, name="columns")
         for b in range(BLOCKS):
@@ -76,28 +81,37 @@ def tile_block_kernel(tc, x, attn, bn_mean, bn_var, bn_g, bn_b, offs, out):
         nc.vector.tensor_mul(scaled_mean[:], running_mean, scale[:])
         nc.vector.tensor_sub(bias[:], shift, scaled_mean[:])
 
+        sums = []
+        means = []
         for b in range(BLOCKS):
-            summed = work.tile([P, ENTRIES], F32, name="summed")
-            partial = work_psum.tile([P, CENTRES, LANES], F32, name="partial")
-            for k in range(PIECES):
-                entries = slice(k * PIECE, (k + 1) * PIECE)
-                piece = offsets[:, k * PIECE // PER_COLUMN : (k + 1) * PIECE // PER_COLUMN]
+            summed = held.tile([P, ENTRIES], F32, name=f"summed{b}")
+            partial = held_psum.tile([P, CENTRES, LANES], F32, name=f"partial{b}")
+            for first, end in pieces_of(b):
+                entries = slice(first, end)
+                piece = offsets[:, first // PER_COLUMN : end // PER_COLUMN]
                 nc.vector.tensor_tensor(
                     summed[:, entries], stores[b][:].indirect(piece), branches[b][:, entries], ALU.add
                 )
                 runs = summed[:, entries].rearrange("p (t s l) -> p s t l", s=STEPS, l=LANES)
-                centres = slice(k * PIECE_CENTRES, (k + 1) * PIECE_CENTRES)
+                centres = slice(first // GROUP, end // GROUP)
                 for s in range(STEPS):
                     nc.tensor.matmul(
-                        partial[:, centres, :], averager[:], runs[:, s], start=(s == 0), stop=(s == STEPS - 1)
+                        partial[:, centres, :], identity[:], runs[:, s], start=(s == 0), stop=(s == STEPS - 1)
                     )
 
+            lanes = held.tile([P, CENTRES, LANES], F32, name=f"lanes{b}")
+            nc.scalar.mul(lanes[:], partial[:], 1.0 / GROUP)
+            sums.append(summed)
+            means.append(lanes)
+
+        for b in range(BLOCKS):
             largest = work.tile([P, CENTRES], F32, name="largest")
-            average = work.tile([P, CENTRES], F32, name="average")
-            pooled = work.tile([P, CENTRES], F32, name="pooled")
-            nc.vector.tensor_reduce(largest[:], summed[:].rearrange("p (t r) -> p t r", r=GROUP), AXIS_X, ALU.max)
-            nc.vector.tensor_reduce(average[:], partial[:], AXIS_X, ALU.add)
-            nc.vector.tensor_add(pooled[:], largest[:], average[:])
+            nc.vector.tensor_reduce(largest[:], sums[b][:].rearrange("p (t r) -> p t r", r=GROUP), AXIS_X, ALU.max)
+
+            pooled = work_psum.tile([P, CENTRES], F32, name="pooled")
+            for l in range(LANES):
+                nc.tensor.matmul(pooled[:], identity[:], means[b][:, :, l], start=(l == 0), stop=False)
+            nc.tensor.matmul(pooled[:], identity[:], largest[:], start=False, stop=True)
 
             result = work.tile([P, CENTRES], F32, name="result")
             nc.scalar.activation(

@@ -40,6 +40,10 @@ def tile_block_kernel(tc, x, attn, bn_mean, bn_var, bn_g, bn_b, offs, out):
         offsets = held.tile([P, ENTRIES // PER_COLUMN], U16, name="offsets")
         nc.sync.dma_start(offsets[:], offs)
 
+        rows = held.tile([PARAMS, CHANNELS], F32, name="rows")
+        for i, vector in enumerate((bn_mean, bn_var, bn_g, bn_b)):
+            nc.scalar.dma_start(rows[i : i + 1, :], vector.rearrange("c o -> o c"))
+
         stores = []
         branches = []
         loads = []
@@ -56,30 +60,8 @@ def tile_block_kernel(tc, x, attn, bn_mean, bn_var, bn_g, bn_b, offs, out):
             queue = nc.sync if n % 2 == 0 else nc.scalar
             queue.dma_start(part, source)
 
-        rows = held.tile([PARAMS, CHANNELS], F32, name="rows")
-        for i, vector in enumerate((bn_mean, bn_var, bn_g, bn_b)):
-            nc.sync.dma_start(rows[i : i + 1, :], vector.rearrange("c o -> o c"))
-
         identity = held.tile([P, P], F32, name="identity")
         make_identity(nc, identity[:])
-
-        columns = held_psum.tile([P, BLOCKS, PARAMS], F32, name="columns")
-        for b in range(BLOCKS):
-            nc.tensor.matmul(
-                columns[:, b, :], rows[:, b * P : (b + 1) * P], identity[:PARAMS, :PARAMS], start=True, stop=True
-            )
-        running_mean, running_var, gain, shift = (columns[:, :, i] for i in range(PARAMS))
-
-        deviation = held.tile([P, BLOCKS], F32, name="deviation")
-        inverse = held.tile([P, BLOCKS], F32, name="inverse")
-        scale = held.tile([P, BLOCKS], F32, name="scale")
-        scaled_mean = held.tile([P, BLOCKS], F32, name="scaled_mean")
-        bias = held.tile([P, BLOCKS], F32, name="bias")
-        nc.scalar.activation(deviation[:], running_var, ACT.Sqrt, bias=EPS)
-        nc.vector.reciprocal(inverse[:], deviation[:])
-        nc.vector.tensor_mul(scale[:], gain, inverse[:])
-        nc.vector.tensor_mul(scaled_mean[:], running_mean, scale[:])
-        nc.vector.tensor_sub(bias[:], shift, scaled_mean[:])
 
         sums = []
         means = []
@@ -103,6 +85,24 @@ def tile_block_kernel(tc, x, attn, bn_mean, bn_var, bn_g, bn_b, offs, out):
             nc.scalar.mul(lanes[:], partial[:], 1.0 / GROUP)
             sums.append(summed)
             means.append(lanes)
+
+        columns = held_psum.tile([P, BLOCKS, PARAMS], F32, name="columns")
+        for b in range(BLOCKS):
+            nc.tensor.matmul(
+                columns[:, b, :], rows[:, b * P : (b + 1) * P], identity[:PARAMS, :PARAMS], start=True, stop=True
+            )
+        running_mean, running_var, gain, shift = (columns[:, :, i] for i in range(PARAMS))
+
+        deviation = held.tile([P, BLOCKS], F32, name="deviation")
+        inverse = held.tile([P, BLOCKS], F32, name="inverse")
+        scale = held.tile([P, BLOCKS], F32, name="scale")
+        scaled_mean = held.tile([P, BLOCKS], F32, name="scaled_mean")
+        bias = held.tile([P, BLOCKS], F32, name="bias")
+        nc.scalar.activation(deviation[:], running_var, ACT.Sqrt, bias=EPS)
+        nc.vector.reciprocal(inverse[:], deviation[:])
+        nc.vector.tensor_mul(scale[:], gain, inverse[:])
+        nc.vector.tensor_mul(scaled_mean[:], running_mean, scale[:])
+        nc.vector.tensor_sub(bias[:], shift, scaled_mean[:])
 
         for b in range(BLOCKS):
             largest = work.tile([P, CENTRES], F32, name="largest")

@@ -40,10 +40,6 @@ def tile_block_kernel(tc, x, attn, bn_mean, bn_var, bn_g, bn_b, offs, out):
         offsets = held.tile([P, ENTRIES // PER_COLUMN], U16, name="offsets")
         nc.sync.dma_start(offsets[:], offs)
 
-        rows = held.tile([PARAMS, CHANNELS], F32, name="rows")
-        for i, vector in enumerate((bn_mean, bn_var, bn_g, bn_b)):
-            nc.scalar.dma_start(rows[i : i + 1, :], vector.rearrange("c o -> o c"))
-
         stores = []
         branches = []
         loads = []
@@ -62,6 +58,28 @@ def tile_block_kernel(tc, x, attn, bn_mean, bn_var, bn_g, bn_b, offs, out):
 
         identity = held.tile([P, P], F32, name="identity")
         make_identity(nc, identity[:])
+
+        rows = held.tile([PARAMS, CHANNELS], F32, name="rows")
+        for i, vector in enumerate((bn_mean, bn_var, bn_g, bn_b)):
+            nc.gpsimd.dma_start(rows[i : i + 1, :], vector.rearrange("c o -> o c"))
+
+        columns = held_psum.tile([P, BLOCKS, PARAMS], F32, name="columns")
+        for b in range(BLOCKS):
+            nc.tensor.matmul(
+                columns[:, b, :], rows[:, b * P : (b + 1) * P], identity[:PARAMS, :PARAMS], start=True, stop=True
+            )
+        running_mean, running_var, gain, shift = (columns[:, :, i] for i in range(PARAMS))
+
+        deviation = held.tile([P, BLOCKS], F32, name="deviation")
+        inverse = held.tile([P, BLOCKS], F32, name="inverse")
+        scale = held.tile([P, BLOCKS], F32, name="scale")
+        scaled_mean = held.tile([P, BLOCKS], F32, name="scaled_mean")
+        bias = held.tile([P, BLOCKS], F32, name="bias")
+        nc.scalar.activation(deviation[:], running_var, ACT.Sqrt, bias=EPS)
+        nc.vector.reciprocal(inverse[:], deviation[:])
+        nc.vector.tensor_mul(scale[:], gain, inverse[:])
+        nc.vector.tensor_mul(scaled_mean[:], running_mean, scale[:])
+        nc.vector.tensor_sub(bias[:], shift, scaled_mean[:])
 
         sums = []
         means = []
@@ -85,24 +103,6 @@ def tile_block_kernel(tc, x, attn, bn_mean, bn_var, bn_g, bn_b, offs, out):
             nc.scalar.mul(lanes[:], partial[:], 1.0 / GROUP)
             sums.append(summed)
             means.append(lanes)
-
-        columns = held_psum.tile([P, BLOCKS, PARAMS], F32, name="columns")
-        for b in range(BLOCKS):
-            nc.tensor.matmul(
-                columns[:, b, :], rows[:, b * P : (b + 1) * P], identity[:PARAMS, :PARAMS], start=True, stop=True
-            )
-        running_mean, running_var, gain, shift = (columns[:, :, i] for i in range(PARAMS))
-
-        deviation = held.tile([P, BLOCKS], F32, name="deviation")
-        inverse = held.tile([P, BLOCKS], F32, name="inverse")
-        scale = held.tile([P, BLOCKS], F32, name="scale")
-        scaled_mean = held.tile([P, BLOCKS], F32, name="scaled_mean")
-        bias = held.tile([P, BLOCKS], F32, name="bias")
-        nc.scalar.activation(deviation[:], running_var, ACT.Sqrt, bias=EPS)
-        nc.vector.reciprocal(inverse[:], deviation[:])
-        nc.vector.tensor_mul(scale[:], gain, inverse[:])
-        nc.vector.tensor_mul(scaled_mean[:], running_mean, scale[:])
-        nc.vector.tensor_sub(bias[:], shift, scaled_mean[:])
 
         for b in range(BLOCKS):
             largest = work.tile([P, CENTRES], F32, name="largest")

@@ -18,6 +18,7 @@ CENTRES = ENTRIES // GROUP
 CUTS = (0, 1024, 2048, 3072, 4096)
 FIRST_CUTS = (0, 256) + CUTS[1:]
 LANES = 4
+SPAN_CENTRES = 64
 STEPS = GROUP // LANES
 EPS = 1e-5
 PARAMS = 4
@@ -92,15 +93,16 @@ def tile_block_kernel(tc, x, attn, bn_mean, bn_var, bn_g, bn_b, offs, out):
                 nc.vector.tensor_tensor(
                     summed[:, entries], stores[b][:].indirect(piece), branches[b][:, entries], ALU.add
                 )
-                runs = summed[:, entries].rearrange("p (t s l) -> p s t l", s=STEPS, l=LANES)
-                centres = slice(first // GROUP, end // GROUP)
+            runs = summed[:].rearrange("p (t s l) -> p s t l", s=STEPS, l=LANES)
+            for first_centre in range(0, CENTRES, SPAN_CENTRES):
+                centres = slice(first_centre, first_centre + SPAN_CENTRES)
                 for s in range(STEPS):
                     nc.tensor.matmul(
-                        partial[:, centres, :], identity[:], runs[:, s], start=(s == 0), stop=(s == STEPS - 1)
+                        partial[:, centres, :], identity[:], runs[:, s, centres, :], start=(s == 0), stop=(s == STEPS - 1)
                     )
 
-            lanes = held.tile([P, CENTRES, LANES], F32, name=f"lanes{b}")
-            nc.scalar.mul(lanes[:], partial[:], 1.0 / GROUP)
+            lanes = held.tile([P, LANES, CENTRES], F32, name=f"lanes{b}")
+            nc.scalar.mul(lanes[:], partial[:].rearrange("p t l -> p l t"), 1.0 / GROUP)
             sums.append(summed)
             means.append(lanes)
 
@@ -110,7 +112,7 @@ def tile_block_kernel(tc, x, attn, bn_mean, bn_var, bn_g, bn_b, offs, out):
 
             pooled = work_psum.tile([P, CENTRES], F32, name="pooled")
             for l in range(LANES):
-                nc.tensor.matmul(pooled[:], identity[:], means[b][:, :, l], start=(l == 0), stop=False)
+                nc.tensor.matmul(pooled[:], identity[:], means[b][:, l, :], start=(l == 0), stop=False)
             nc.tensor.matmul(pooled[:], identity[:], largest[:], start=False, stop=True)
 
             result = work.tile([P, CENTRES], F32, name="result")

@@ -20,6 +20,7 @@ FIRST_CUTS = (0, 256) + CUTS[1:]
 LANES = 4
 SPAN_CENTRES = 64
 STEPS = GROUP // LANES
+HELPED = 64
 EPS = 1e-5
 PARAMS = 4
 FLOPS = 3 * CHANNELS * ENTRIES
@@ -106,14 +107,30 @@ def tile_block_kernel(tc, x, attn, bn_mean, bn_var, bn_g, bn_b, offs, out):
             sums.append(summed)
             means.append(lanes)
 
+        helped = slice(CENTRES - HELPED, CENTRES)
+        halves = sums[BLOCKS - 1][:].rearrange("p (t h r) -> p t h r", h=2, r=GROUP // 2)
+        difference = held.tile([P, HELPED, GROUP // 2], F32, name="difference")
+        excess = held.tile([P, HELPED, GROUP // 2], F32, name="excess")
+        better = held.tile([P, HELPED, GROUP // 2], F32, name="better")
+        nc.gpsimd.tensor_tensor(difference[:], halves[:, helped, 0, :], halves[:, helped, 1, :], ALU.subtract)
+        nc.scalar.activation(excess[:], difference[:], ACT.Relu)
+        nc.gpsimd.tensor_tensor(better[:], halves[:, helped, 1, :], excess[:], ALU.add)
+
         for b in range(BLOCKS):
             largest = work.tile([P, CENTRES], F32, name="largest")
-            nc.vector.tensor_reduce(largest[:], sums[b][:].rearrange("p (t r) -> p t r", r=GROUP), AXIS_X, ALU.max)
+            members = sums[b][:].rearrange("p (t r) -> p t r", r=GROUP)
+            if b < BLOCKS - 1:
+                nc.vector.tensor_reduce(largest[:], members, AXIS_X, ALU.max)
+            else:
+                alone = slice(0, CENTRES - HELPED)
+                nc.vector.tensor_reduce(largest[:, alone], members[:, alone, :], AXIS_X, ALU.max)
+                nc.vector.tensor_reduce(largest[:, helped], better[:], AXIS_X, ALU.max)
 
-            pooled = work_psum.tile([P, CENTRES], F32, name="pooled")
+            mean = work_psum.tile([P, CENTRES], F32, name="mean")
             for l in range(LANES):
-                nc.tensor.matmul(pooled[:], identity[:], means[b][:, l, :], start=(l == 0), stop=False)
-            nc.tensor.matmul(pooled[:], identity[:], largest[:], start=False, stop=True)
+                nc.tensor.matmul(mean[:], identity[:], means[b][:, l, :], start=(l == 0), stop=(l == LANES - 1))
+            pooled = work.tile([P, CENTRES], F32, name="pooled")
+            nc.vector.tensor_add(pooled[:], largest[:], mean[:])
 
             result = work.tile([P, CENTRES], F32, name="result")
             nc.scalar.activation(

@@ -18,7 +18,8 @@ CENTRES = ENTRIES // GROUP
 CUTS = (0, 1024, 2048, 3072, 4096)
 FIRST_CUTS = (0, 256) + CUTS[1:]
 LANES = 4
-SPAN_CENTRES = 64
+SPANS = (0, 64, 128)
+FIRST_SPANS = (0, 32, 64, 128)
 STEPS = GROUP // LANES
 HELPED = 64
 EPS = 1e-5
@@ -29,6 +30,11 @@ FLOPS = 3 * CHANNELS * ENTRIES
 def pieces_of(b):
     cuts = FIRST_CUTS if b == 0 else CUTS
     return list(zip(cuts[:-1], cuts[1:]))
+
+
+def spans_of(b):
+    spans = FIRST_SPANS if b == 0 else SPANS
+    return list(zip(spans[:-1], spans[1:]))
 
 
 def tile_block_kernel(tc, x, attn, bn_mean, bn_var, bn_g, bn_b, offs, out):
@@ -94,12 +100,13 @@ def tile_block_kernel(tc, x, attn, bn_mean, bn_var, bn_g, bn_b, offs, out):
                 nc.vector.tensor_tensor(
                     summed[:, entries], stores[b][:].indirect(piece), branches[b][:, entries], ALU.add
                 )
-            runs = summed[:].rearrange("p (t s l) -> p s t l", s=STEPS, l=LANES)
-            for first_centre in range(0, CENTRES, SPAN_CENTRES):
-                centres = slice(first_centre, first_centre + SPAN_CENTRES)
+            for first_centre, end_centre in spans_of(b):
+                centres = slice(first_centre, end_centre)
+                span = summed[:, first_centre * GROUP : end_centre * GROUP]
+                runs = span.rearrange("p (t s l) -> p s t l", s=STEPS, l=LANES)
                 for s in range(STEPS):
                     nc.tensor.matmul(
-                        partial[:, centres, :], identity[:], runs[:, s, centres, :], start=(s == 0), stop=(s == STEPS - 1)
+                        partial[:, centres, :], identity[:], runs[:, s], start=(s == 0), stop=(s == STEPS - 1)
                     )
 
             lanes = held.tile([P, LANES, CENTRES], F32, name=f"lanes{b}")
@@ -112,9 +119,14 @@ def tile_block_kernel(tc, x, attn, bn_mean, bn_var, bn_g, bn_b, offs, out):
         difference = held.tile([P, HELPED, GROUP // 2], F32, name="difference")
         excess = held.tile([P, HELPED, GROUP // 2], F32, name="excess")
         better = held.tile([P, HELPED, GROUP // 2], F32, name="better")
-        nc.gpsimd.tensor_tensor(difference[:], halves[:, helped, 0, :], halves[:, helped, 1, :], ALU.subtract)
-        nc.scalar.activation(excess[:], difference[:], ACT.Relu)
-        nc.gpsimd.tensor_tensor(better[:], halves[:, helped, 1, :], excess[:], ALU.add)
+        parts = (slice(0, GROUP // 4), slice(GROUP // 4, GROUP // 2))
+        for part in parts:
+            nc.gpsimd.tensor_tensor(
+                difference[:, :, part], halves[:, helped, 0, part], halves[:, helped, 1, part], ALU.subtract
+            )
+            nc.scalar.activation(excess[:, :, part], difference[:, :, part], ACT.Relu)
+        for part in parts:
+            nc.gpsimd.tensor_tensor(better[:, :, part], halves[:, helped, 1, part], excess[:, :, part], ALU.add)
 
         for b in range(BLOCKS):
             largest = work.tile([P, CENTRES], F32, name="largest")

@@ -60,16 +60,16 @@ def tile_block_kernel(tc, x, attn, bn_mean, bn_var, bn_g, bn_b, offs, out):
                 loads.append((branch[:, first:end], attn[channels, first:end]))
             stores.append(store)
             branches.append(branch)
+        rows = held.tile([PARAMS, CHANNELS], F32, name="rows")
         for n, (part, source) in enumerate(loads):
             queue = nc.sync if n % 2 == 0 else nc.scalar
             queue.dma_start(part, source)
+            if n == 0:
+                for i, vector in enumerate((bn_mean, bn_var, bn_g, bn_b)):
+                    nc.sync.dma_start(rows[i : i + 1, :], vector.rearrange("c o -> o c"))
 
         identity = held.tile([P, P], F32, name="identity")
         make_identity(nc, identity[:])
-
-        rows = held.tile([PARAMS, CHANNELS], F32, name="rows")
-        for i, vector in enumerate((bn_mean, bn_var, bn_g, bn_b)):
-            nc.gpsimd.dma_start(rows[i : i + 1, :], vector.rearrange("c o -> o c"))
 
         columns = held_psum.tile([P, BLOCKS, PARAMS], F32, name="columns")
         for b in range(BLOCKS):

@@ -17,10 +17,7 @@ GROUP = 32
 CENTRES = ENTRIES // GROUP
 CUTS = (0, 1024, 2048, 3072, 4096)
 FIRST_CUTS = (0, 256) + CUTS[1:]
-LANES = 4
-SPANS = (0, 64, 128)
-FIRST_SPANS = (0, 32, 64, 128)
-STEPS = GROUP // LANES
+BANK = 512
 HELPED = 64
 EPS = 1e-5
 PARAMS = 4
@@ -30,11 +27,6 @@ FLOPS = 3 * CHANNELS * ENTRIES
 def pieces_of(b):
     cuts = FIRST_CUTS if b == 0 else CUTS
     return list(zip(cuts[:-1], cuts[1:]))
-
-
-def spans_of(b):
-    spans = FIRST_SPANS if b == 0 else SPANS
-    return list(zip(spans[:-1], spans[1:]))
 
 
 def tile_block_kernel(tc, x, attn, bn_mean, bn_var, bn_g, bn_b, offs, out):
@@ -93,26 +85,23 @@ def tile_block_kernel(tc, x, attn, bn_mean, bn_var, bn_g, bn_b, offs, out):
         means = []
         for b in range(BLOCKS):
             summed = held.tile([P, ENTRIES], F32, name=f"summed{b}")
-            partial = held_psum.tile([P, CENTRES, LANES], F32, name=f"partial{b}")
+            total = held_psum.tile([P, BANK], F32, name=f"total{b}")
             for first, end in pieces_of(b):
                 entries = slice(first, end)
                 piece = offsets[:, first // PER_COLUMN : end // PER_COLUMN]
                 nc.vector.tensor_tensor(
                     summed[:, entries], stores[b][:].indirect(piece), branches[b][:, entries], ALU.add
                 )
-            for first_centre, end_centre in spans_of(b):
-                centres = slice(first_centre, end_centre)
-                span = summed[:, first_centre * GROUP : end_centre * GROUP]
-                runs = span.rearrange("p (t s l) -> p s t l", s=STEPS, l=LANES)
-                for s in range(STEPS):
-                    nc.tensor.matmul(
-                        partial[:, centres, :], identity[:], runs[:, s], start=(s == 0), stop=(s == STEPS - 1)
-                    )
+            by_member = summed[:].rearrange("p (t r) -> p r t", r=GROUP)
+            for r in range(GROUP):
+                nc.tensor.matmul(
+                    total[:, :P], by_member[:, r, :], identity[:], is_transpose=True, start=(r == 0), stop=(r == GROUP - 1)
+                )
 
-            lanes = held.tile([P, LANES, CENTRES], F32, name=f"lanes{b}")
-            nc.scalar.mul(lanes[:], partial[:].rearrange("p t l -> p l t"), 1.0 / GROUP)
+            flipped = held.tile([P, P], F32, name=f"flipped{b}")
+            nc.scalar.mul(flipped[:], total[:, :P], 1.0 / GROUP)
             sums.append(summed)
-            means.append(lanes)
+            means.append(flipped)
 
         helped = slice(CENTRES - HELPED, CENTRES)
         halves = sums[BLOCKS - 1][:].rearrange("p (t h r) -> p t h r", h=2, r=GROUP // 2)
@@ -139,8 +128,7 @@ def tile_block_kernel(tc, x, attn, bn_mean, bn_var, bn_g, bn_b, offs, out):
                 nc.vector.tensor_reduce(largest[:, helped], better[:], AXIS_X, ALU.max)
 
             mean = work_psum.tile([P, CENTRES], F32, name="mean")
-            for l in range(LANES):
-                nc.tensor.matmul(mean[:], identity[:], means[b][:, l, :], start=(l == 0), stop=(l == LANES - 1))
+            nc.tensor.transpose(mean[:], means[b][:], identity[:])
             pooled = work.tile([P, CENTRES], F32, name="pooled")
             nc.vector.tensor_add(pooled[:], largest[:], mean[:])
 

@@ -15,18 +15,24 @@ ENTRIES = 4096
 PER_COLUMN = 16
 GROUP = 32
 CENTRES = ENTRIES // GROUP
-CUTS = (0, 1024, 2048, 3072, 4096)
-FIRST_CUTS = (0, 256) + CUTS[1:]
-BANK = 512
-HELPED = 64
+QUARTER = 1024
+QUARTERS = ENTRIES // QUARTER
+QUARTER_CENTRES = QUARTER // GROUP
+PAIRS = QUARTER // 2
+CHUNKS = PAIRS // P
+FIRST_PIECE = 256
+HELPED = 7
+SHARE = GROUP // QUARTERS
 EPS = 1e-5
 PARAMS = 4
 FLOPS = 3 * CHANNELS * ENTRIES
 
 
-def pieces_of(b):
-    cuts = FIRST_CUTS if b == 0 else CUTS
-    return list(zip(cuts[:-1], cuts[1:]))
+def pieces_of(b, k):
+    first, end = k * QUARTER, (k + 1) * QUARTER
+    if b == 0 and k == 0:
+        return [(first, FIRST_PIECE), (FIRST_PIECE, end)]
+    return [(first, end)]
 
 
 def tile_block_kernel(tc, x, attn, bn_mean, bn_var, bn_g, bn_b, offs, out):
@@ -34,8 +40,9 @@ def tile_block_kernel(tc, x, attn, bn_mean, bn_var, bn_g, bn_b, offs, out):
     with (
         tc.tile_pool(name="held", bufs=1) as held,
         tc.psum_pool(name="held_psum", bufs=1) as held_psum,
+        tc.tile_pool(name="road", bufs=3) as road,
+        tc.psum_pool(name="road_psum", bufs=2) as road_psum,
         tc.tile_pool(name="work", bufs=BLOCKS) as work,
-        tc.psum_pool(name="work_psum", bufs=BLOCKS) as work_psum,
     ):
         offsets = held.tile([P, ENTRIES // PER_COLUMN], U16, name="offsets")
         nc.sync.dma_start(offsets[:], offs)
@@ -48,8 +55,9 @@ def tile_block_kernel(tc, x, attn, bn_mean, bn_var, bn_g, bn_b, offs, out):
             store = held.tile([P, STORE], F32, name=f"store{b}")
             loads.append((store[:], x[channels, :]))
             branch = held.tile([P, ENTRIES], F32, name=f"branch{b}")
-            for first, end in pieces_of(b):
-                loads.append((branch[:, first:end], attn[channels, first:end]))
+            for k in range(QUARTERS):
+                for first, end in pieces_of(b, k):
+                    loads.append((branch[:, first:end], attn[channels, first:end]))
             stores.append(store)
             branches.append(branch)
         rows = held.tile([PARAMS, CHANNELS], F32, name="rows")
@@ -62,6 +70,8 @@ def tile_block_kernel(tc, x, attn, bn_mean, bn_var, bn_g, bn_b, offs, out):
 
         identity = held.tile([P, P], F32, name="identity")
         make_identity(nc, identity[:])
+        minus_identity = held.tile([P, P], F32, name="minus_identity")
+        nc.gpsimd.tensor_scalar_mul(minus_identity[:], identity[:], -1.0)
 
         columns = held_psum.tile([P, BLOCKS, PARAMS], F32, name="columns")
         for b in range(BLOCKS):
@@ -81,59 +91,106 @@ def tile_block_kernel(tc, x, attn, bn_mean, bn_var, bn_g, bn_b, offs, out):
         nc.vector.tensor_mul(scaled_mean[:], running_mean, scale[:])
         nc.vector.tensor_sub(bias[:], shift, scaled_mean[:])
 
-        sums = []
-        means = []
-        for b in range(BLOCKS):
-            summed = held.tile([P, ENTRIES], F32, name=f"summed{b}")
-            total = held_psum.tile([P, BANK], F32, name=f"total{b}")
-            for first, end in pieces_of(b):
+        sums = [held.tile([P, ENTRIES], F32, name=f"summed{b}") for b in range(BLOCKS)]
+        maxima = [held.tile([P, CENTRES], F32, name=f"largest{b}") for b in range(BLOCKS)]
+        negatives = {}
+        differences = {}
+        sums_back = {}
+        winners = {}
+        totals = {}
+        means = {}
+
+        def quarter_of(u):
+            b, k = divmod(u, QUARTERS)
+            return sums[b][:, k * QUARTER : (k + 1) * QUARTER]
+
+        def look_up(u):
+            b, k = divmod(u, QUARTERS)
+            for first, end in pieces_of(b, k):
                 entries = slice(first, end)
                 piece = offsets[:, first // PER_COLUMN : end // PER_COLUMN]
                 nc.vector.tensor_tensor(
-                    summed[:, entries], stores[b][:].indirect(piece), branches[b][:, entries], ALU.add
+                    sums[b][:, entries], stores[b][:].indirect(piece), branches[b][:, entries], ALU.add
                 )
-            by_member = summed[:].rearrange("p (t r) -> p r t", r=GROUP)
-            for r in range(GROUP):
+
+        def subtract(u):
+            pairs = quarter_of(u).rearrange("p (n two) -> p two n", two=2)
+            negative = road.tile([P, PAIRS], F32, name="negative")
+            nc.scalar.mul(negative[:], pairs[:, 1, :], -1.0)
+            difference = road_psum.tile([P, PAIRS], F32, name="difference")
+            for q in range(CHUNKS):
+                chunk = slice(q * P, (q + 1) * P)
                 nc.tensor.matmul(
-                    total[:, :P], by_member[:, r, :], identity[:], is_transpose=True, start=(r == 0), stop=(r == GROUP - 1)
+                    difference[:, chunk], pairs[:, 0, chunk], identity[:], is_transpose=True, start=True, stop=False
                 )
+                nc.tensor.matmul(
+                    difference[:, chunk], negative[:, chunk], identity[:], is_transpose=True, start=False, stop=True
+                )
+            negatives[u] = negative
+            differences[u] = difference
 
-            flipped = held.tile([P, P], F32, name=f"flipped{b}")
-            nc.scalar.mul(flipped[:], total[:, :P], 1.0 / GROUP)
-            sums.append(summed)
-            means.append(flipped)
+        def add_back(u):
+            excess = road.tile([P, PAIRS], F32, name="excess")
+            nc.scalar.activation(excess[:], differences[u][:], ACT.Relu)
+            better = road_psum.tile([P, PAIRS], F32, name="better")
+            nc.tensor.matmul(better[:], minus_identity[:], negatives[u][:], start=True, stop=False)
+            for q in range(CHUNKS):
+                chunk = slice(q * P, (q + 1) * P)
+                nc.tensor.matmul(
+                    better[:, chunk], excess[:, chunk], identity[:], is_transpose=True, start=False, stop=(q == CHUNKS - 1)
+                )
+            sums_back[u] = better
 
-        helped = slice(CENTRES - HELPED, CENTRES)
-        halves = sums[BLOCKS - 1][:].rearrange("p (t h r) -> p t h r", h=2, r=GROUP // 2)
-        difference = held.tile([P, HELPED, GROUP // 2], F32, name="difference")
-        excess = held.tile([P, HELPED, GROUP // 2], F32, name="excess")
-        better = held.tile([P, HELPED, GROUP // 2], F32, name="better")
-        parts = (slice(0, GROUP // 4), slice(GROUP // 4, GROUP // 2))
-        for part in parts:
-            nc.gpsimd.tensor_tensor(
-                difference[:, :, part], halves[:, helped, 0, part], halves[:, helped, 1, part], ALU.subtract
-            )
-            nc.scalar.activation(excess[:, :, part], difference[:, :, part], ACT.Relu)
-        for part in parts:
-            nc.gpsimd.tensor_tensor(better[:, :, part], halves[:, helped, 1, part], excess[:, :, part], ALU.add)
+        def park(u):
+            winners[u] = held.tile([P, PAIRS], F32, name=f"winners{u}")
+            nc.scalar.copy(winners[u][:], sums_back[u][:])
 
-        for b in range(BLOCKS):
-            largest = work.tile([P, CENTRES], F32, name="largest")
-            members = sums[b][:].rearrange("p (t r) -> p t r", r=GROUP)
-            if b < BLOCKS - 1:
-                nc.vector.tensor_reduce(largest[:], members, AXIS_X, ALU.max)
+        def take_max(u):
+            b, k = divmod(u, QUARTERS)
+            centres = slice(k * QUARTER_CENTRES, (k + 1) * QUARTER_CENTRES)
+            if u in winners:
+                candidates = winners[u][:].rearrange("p (t r) -> p t r", r=GROUP // 2)
             else:
-                alone = slice(0, CENTRES - HELPED)
-                nc.vector.tensor_reduce(largest[:, alone], members[:, alone, :], AXIS_X, ALU.max)
-                nc.vector.tensor_reduce(largest[:, helped], better[:], AXIS_X, ALU.max)
+                candidates = quarter_of(u).rearrange("p (t r) -> p t r", r=GROUP)
+            nc.vector.tensor_reduce(maxima[b][:, centres], candidates, AXIS_X, ALU.max)
 
-            mean = work_psum.tile([P, CENTRES], F32, name="mean")
+        def add_members(b, share):
+            if share == 0:
+                totals[b] = held_psum.tile([P, P], F32, name="total")
+            by_member = sums[b][:].rearrange("p (t r) -> p r t", r=GROUP)
+            for r in range(share * SHARE, (share + 1) * SHARE):
+                nc.tensor.matmul(
+                    totals[b][:], by_member[:, r, :], identity[:], is_transpose=True, start=(r == 0), stop=(r == GROUP - 1)
+                )
+            if share == QUARTERS - 1:
+                means[b] = work.tile([P, P], F32, name="flipped")
+                nc.scalar.mul(means[b][:], totals[b][:], 1.0 / GROUP)
+
+        def finish(b):
+            mean = held_psum.tile([P, CENTRES], F32, name="mean")
             nc.tensor.transpose(mean[:], means[b][:], identity[:])
             pooled = work.tile([P, CENTRES], F32, name="pooled")
-            nc.vector.tensor_add(pooled[:], largest[:], mean[:])
-
+            nc.vector.tensor_add(pooled[:], maxima[b][:], mean[:])
             result = work.tile([P, CENTRES], F32, name="result")
             nc.scalar.activation(
                 result[:], pooled[:], ACT.Gelu, bias=bias[:, b : b + 1], scale=scale[:, b : b + 1]
             )
             nc.sync.dma_start(out[b * P : (b + 1) * P, :], result[:])
+
+        units = BLOCKS * QUARTERS
+        for step in range(units + QUARTERS):
+            if step < units:
+                look_up(step)
+            if step < HELPED:
+                subtract(step)
+            if 0 <= step - 1 < HELPED:
+                add_back(step - 1)
+            if 0 <= step - 2 < HELPED:
+                park(step - 2)
+            if step >= QUARTERS:
+                add_members(*divmod(step - QUARTERS, QUARTERS))
+
+        for u in range(units):
+            take_max(u)
+            if u % QUARTERS == QUARTERS - 1:
+                finish(u // QUARTERS)

@@ -17,12 +17,9 @@ GROUP = 32
 CENTRES = ENTRIES // GROUP
 QUARTER = 1024
 QUARTERS = ENTRIES // QUARTER
-QUARTER_CENTRES = QUARTER // GROUP
 PAIRS = QUARTER // 2
 CHUNKS = PAIRS // P
 FIRST_PIECE = 256
-HELPED = 7
-SHARE = GROUP // QUARTERS
 EPS = 1e-5
 PARAMS = 4
 FLOPS = 3 * CHANNELS * ENTRIES
@@ -43,6 +40,7 @@ def tile_block_kernel(tc, x, attn, bn_mean, bn_var, bn_g, bn_b, offs, out):
         tc.tile_pool(name="road", bufs=3) as road,
         tc.psum_pool(name="road_psum", bufs=2) as road_psum,
         tc.tile_pool(name="work", bufs=BLOCKS) as work,
+        tc.psum_pool(name="work_psum", bufs=BLOCKS) as work_psum,
     ):
         offsets = held.tile([P, ENTRIES // PER_COLUMN], U16, name="offsets")
         nc.sync.dma_start(offsets[:], offs)
@@ -73,7 +71,7 @@ def tile_block_kernel(tc, x, attn, bn_mean, bn_var, bn_g, bn_b, offs, out):
         minus_identity = held.tile([P, P], F32, name="minus_identity")
         nc.gpsimd.tensor_scalar_mul(minus_identity[:], identity[:], -1.0)
 
-        columns = held_psum.tile([P, BLOCKS, PARAMS], F32, name="columns")
+        columns = work_psum.tile([P, BLOCKS, PARAMS], F32, name="columns", tag="small")
         for b in range(BLOCKS):
             nc.tensor.matmul(
                 columns[:, b, :], rows[:, b * P : (b + 1) * P], identity[:PARAMS, :PARAMS], start=True, stop=True
@@ -92,20 +90,9 @@ def tile_block_kernel(tc, x, attn, bn_mean, bn_var, bn_g, bn_b, offs, out):
         nc.vector.tensor_sub(bias[:], shift, scaled_mean[:])
 
         sums = [held.tile([P, ENTRIES], F32, name=f"summed{b}") for b in range(BLOCKS)]
-        maxima = [held.tile([P, CENTRES], F32, name=f"largest{b}") for b in range(BLOCKS)]
-        negatives = {}
-        differences = {}
-        sums_back = {}
-        winners = {}
-        totals = {}
-        means = {}
+        winners = held.tile([P, ENTRIES // 2], F32, name="winners")
 
-        def quarter_of(u):
-            b, k = divmod(u, QUARTERS)
-            return sums[b][:, k * QUARTER : (k + 1) * QUARTER]
-
-        def look_up(u):
-            b, k = divmod(u, QUARTERS)
+        def look_up(b, k):
             for first, end in pieces_of(b, k):
                 entries = slice(first, end)
                 piece = offsets[:, first // PER_COLUMN : end // PER_COLUMN]
@@ -113,8 +100,8 @@ def tile_block_kernel(tc, x, attn, bn_mean, bn_var, bn_g, bn_b, offs, out):
                     sums[b][:, entries], stores[b][:].indirect(piece), branches[b][:, entries], ALU.add
                 )
 
-        def subtract(u):
-            pairs = quarter_of(u).rearrange("p (n two) -> p two n", two=2)
+        def first_round(k):
+            pairs = sums[0][:, k * QUARTER : (k + 1) * QUARTER].rearrange("p (n two) -> p two n", two=2)
             negative = road.tile([P, PAIRS], F32, name="negative")
             nc.scalar.mul(negative[:], pairs[:, 1, :], -1.0)
             difference = road_psum.tile([P, PAIRS], F32, name="difference")
@@ -126,71 +113,49 @@ def tile_block_kernel(tc, x, attn, bn_mean, bn_var, bn_g, bn_b, offs, out):
                 nc.tensor.matmul(
                     difference[:, chunk], negative[:, chunk], identity[:], is_transpose=True, start=False, stop=True
                 )
-            negatives[u] = negative
-            differences[u] = difference
-
-        def add_back(u):
             excess = road.tile([P, PAIRS], F32, name="excess")
-            nc.scalar.activation(excess[:], differences[u][:], ACT.Relu)
+            nc.scalar.activation(excess[:], difference[:], ACT.Relu)
             better = road_psum.tile([P, PAIRS], F32, name="better")
-            nc.tensor.matmul(better[:], minus_identity[:], negatives[u][:], start=True, stop=False)
+            nc.tensor.matmul(better[:], minus_identity[:], negative[:], start=True, stop=False)
             for q in range(CHUNKS):
                 chunk = slice(q * P, (q + 1) * P)
                 nc.tensor.matmul(
                     better[:, chunk], excess[:, chunk], identity[:], is_transpose=True, start=False, stop=(q == CHUNKS - 1)
                 )
-            sums_back[u] = better
+            nc.scalar.copy(winners[:, k * PAIRS : (k + 1) * PAIRS], better[:])
 
-        def park(u):
-            winners[u] = held.tile([P, PAIRS], F32, name=f"winners{u}")
-            nc.scalar.copy(winners[u][:], sums_back[u][:])
-
-        def take_max(u):
-            b, k = divmod(u, QUARTERS)
-            centres = slice(k * QUARTER_CENTRES, (k + 1) * QUARTER_CENTRES)
-            if u in winners:
-                candidates = winners[u][:].rearrange("p (t r) -> p t r", r=GROUP // 2)
-            else:
-                candidates = quarter_of(u).rearrange("p (t r) -> p t r", r=GROUP)
-            nc.vector.tensor_reduce(maxima[b][:, centres], candidates, AXIS_X, ALU.max)
-
-        def add_members(b, share):
-            if share == 0:
-                totals[b] = held_psum.tile([P, P], F32, name="total")
+        def flipped_mean(b):
+            total = held_psum.tile([P, P], F32, name="total")
             by_member = sums[b][:].rearrange("p (t r) -> p r t", r=GROUP)
-            for r in range(share * SHARE, (share + 1) * SHARE):
+            for r in range(GROUP):
                 nc.tensor.matmul(
-                    totals[b][:], by_member[:, r, :], identity[:], is_transpose=True, start=(r == 0), stop=(r == GROUP - 1)
+                    total[:], by_member[:, r, :], identity[:], is_transpose=True, start=(r == 0), stop=(r == GROUP - 1)
                 )
-            if share == QUARTERS - 1:
-                means[b] = work.tile([P, P], F32, name="flipped")
-                nc.scalar.mul(means[b][:], totals[b][:], 1.0 / GROUP)
+            flipped = work.tile([P, P], F32, name="flipped")
+            nc.scalar.mul(flipped[:], total[:], 1.0 / GROUP)
+            return flipped
 
-        def finish(b):
-            mean = held_psum.tile([P, CENTRES], F32, name="mean")
-            nc.tensor.transpose(mean[:], means[b][:], identity[:])
+        def finish(b, candidates, flipped):
+            largest = work.tile([P, CENTRES], F32, name="largest")
+            nc.vector.tensor_reduce(largest[:], candidates, AXIS_X, ALU.max)
+            mean = work_psum.tile([P, CENTRES], F32, name="mean", tag="small")
+            nc.tensor.transpose(mean[:], flipped[:], identity[:])
             pooled = work.tile([P, CENTRES], F32, name="pooled")
-            nc.vector.tensor_add(pooled[:], maxima[b][:], mean[:])
+            nc.vector.tensor_add(pooled[:], largest[:], mean[:])
             result = work.tile([P, CENTRES], F32, name="result")
             nc.scalar.activation(
                 result[:], pooled[:], ACT.Gelu, bias=bias[:, b : b + 1], scale=scale[:, b : b + 1]
             )
             nc.sync.dma_start(out[b * P : (b + 1) * P, :], result[:])
 
-        units = BLOCKS * QUARTERS
-        for step in range(units + QUARTERS):
-            if step < units:
-                look_up(step)
-            if step < HELPED:
-                subtract(step)
-            if 0 <= step - 1 < HELPED:
-                add_back(step - 1)
-            if 0 <= step - 2 < HELPED:
-                park(step - 2)
-            if step >= QUARTERS:
-                add_members(*divmod(step - QUARTERS, QUARTERS))
+        means = []
+        for b in range(BLOCKS):
+            for k in range(QUARTERS):
+                look_up(b, k)
+                if b == 0:
+                    first_round(k)
+            means.append(flipped_mean(b))
 
-        for u in range(units):
-            take_max(u)
-            if u % QUARTERS == QUARTERS - 1:
-                finish(u // QUARTERS)
+        finish(1, sums[1][:].rearrange("p (t r) -> p t r", r=GROUP), means[1])
+        finish(0, winners[:].rearrange("p (t r) -> p t r", r=GROUP // 2), means[0])
+        finish(2, sums[2][:].rearrange("p (t r) -> p t r", r=GROUP), means[2])

@@ -39,6 +39,7 @@ def tile_block_kernel(tc, x, attn, bn_mean, bn_var, bn_g, bn_b, offs, out):
         tc.psum_pool(name="held_psum", bufs=1) as held_psum,
         tc.tile_pool(name="road", bufs=3) as road,
         tc.psum_pool(name="road_psum", bufs=2) as road_psum,
+        tc.psum_pool(name="turned_psum", bufs=1) as turned_psum,
         tc.tile_pool(name="work", bufs=BLOCKS) as work,
         tc.psum_pool(name="work_psum", bufs=BLOCKS) as work_psum,
     ):
@@ -68,8 +69,6 @@ def tile_block_kernel(tc, x, attn, bn_mean, bn_var, bn_g, bn_b, offs, out):
 
         identity = held.tile([P, P], F32, name="identity")
         make_identity(nc, identity[:])
-        minus_identity = held.tile([P, P], F32, name="minus_identity")
-        nc.gpsimd.tensor_scalar_mul(minus_identity[:], identity[:], -1.0)
 
         columns = work_psum.tile([P, BLOCKS, PARAMS], F32, name="columns", tag="small")
         for b in range(BLOCKS):
@@ -113,14 +112,22 @@ def tile_block_kernel(tc, x, attn, bn_mean, bn_var, bn_g, bn_b, offs, out):
                 nc.tensor.matmul(
                     difference[:, chunk], negative[:, chunk], identity[:], is_transpose=True, start=False, stop=True
                 )
+            turned = turned_psum.tile([P, PAIRS], F32, name="turned")
+            for q in range(CHUNKS):
+                chunk = slice(q * P, (q + 1) * P)
+                nc.tensor.transpose(turned[:, chunk], negative[:, chunk], identity[:])
             excess = road.tile([P, PAIRS], F32, name="excess")
             nc.scalar.activation(excess[:], difference[:], ACT.Relu)
-            better = road_psum.tile([P, PAIRS], F32, name="better")
-            nc.tensor.matmul(better[:], minus_identity[:], negative[:], start=True, stop=False)
+            second = road.tile([P, PAIRS], F32, name="second")
+            nc.scalar.mul(second[:], turned[:], -1.0)
+            better = turned_psum.tile([P, PAIRS], F32, name="better")
             for q in range(CHUNKS):
                 chunk = slice(q * P, (q + 1) * P)
                 nc.tensor.matmul(
-                    better[:, chunk], excess[:, chunk], identity[:], is_transpose=True, start=False, stop=(q == CHUNKS - 1)
+                    better[:, chunk], excess[:, chunk], identity[:], is_transpose=True, start=True, stop=False
+                )
+                nc.tensor.matmul(
+                    better[:, chunk], second[:, chunk], identity[:], is_transpose=True, start=False, stop=True
                 )
             nc.scalar.copy(winners[:, k * PAIRS : (k + 1) * PAIRS], better[:])
 

@@ -41,7 +41,6 @@ def tile_block_kernel(tc, x, attn, bn_mean, bn_var, bn_g, bn_b, offs, out):
         tc.psum_pool(name="road_psum", bufs=2) as road_psum,
         tc.psum_pool(name="turned_psum", bufs=1) as turned_psum,
         tc.tile_pool(name="work", bufs=BLOCKS) as work,
-        tc.psum_pool(name="work_psum", bufs=BLOCKS) as work_psum,
     ):
         offsets = held.tile([P, ENTRIES // PER_COLUMN], U16, name="offsets")
         nc.sync.dma_start(offsets[:], offs)
@@ -70,26 +69,9 @@ def tile_block_kernel(tc, x, attn, bn_mean, bn_var, bn_g, bn_b, offs, out):
         identity = held.tile([P, P], F32, name="identity")
         make_identity(nc, identity[:])
 
-        columns = work_psum.tile([P, BLOCKS, PARAMS], F32, name="columns", tag="small")
-        for b in range(BLOCKS):
-            nc.tensor.matmul(
-                columns[:, b, :], rows[:, b * P : (b + 1) * P], identity[:PARAMS, :PARAMS], start=True, stop=True
-            )
-        running_mean, running_var, gain, shift = (columns[:, :, i] for i in range(PARAMS))
-
-        deviation = held.tile([P, BLOCKS], F32, name="deviation")
-        inverse = held.tile([P, BLOCKS], F32, name="inverse")
-        scale = held.tile([P, BLOCKS], F32, name="scale")
-        scaled_mean = held.tile([P, BLOCKS], F32, name="scaled_mean")
-        bias = held.tile([P, BLOCKS], F32, name="bias")
-        nc.scalar.activation(deviation[:], running_var, ACT.Sqrt, bias=EPS)
-        nc.vector.reciprocal(inverse[:], deviation[:])
-        nc.vector.tensor_mul(scale[:], gain, inverse[:])
-        nc.vector.tensor_mul(scaled_mean[:], running_mean, scale[:])
-        nc.vector.tensor_sub(bias[:], shift, scaled_mean[:])
-
         sums = [held.tile([P, ENTRIES], F32, name=f"summed{b}") for b in range(BLOCKS)]
         winners = held.tile([P, ENTRIES // 2], F32, name="winners")
+        means = held_psum.tile([P, BLOCKS * CENTRES], F32, name="means")
 
         def look_up(b, k):
             for first, end in pieces_of(b, k):
@@ -131,8 +113,8 @@ def tile_block_kernel(tc, x, attn, bn_mean, bn_var, bn_g, bn_b, offs, out):
                 )
             nc.scalar.copy(winners[:, k * PAIRS : (k + 1) * PAIRS], better[:])
 
-        def flipped_mean(b):
-            total = held_psum.tile([P, P], F32, name="total")
+        def take_mean(b):
+            total = road_psum.tile([P, P], F32, name="total")
             by_member = sums[b][:].rearrange("p (t r) -> p r t", r=GROUP)
             for r in range(GROUP):
                 nc.tensor.matmul(
@@ -140,29 +122,50 @@ def tile_block_kernel(tc, x, attn, bn_mean, bn_var, bn_g, bn_b, offs, out):
                 )
             flipped = work.tile([P, P], F32, name="flipped")
             nc.scalar.mul(flipped[:], total[:], 1.0 / GROUP)
-            return flipped
+            nc.tensor.transpose(means[:, b * CENTRES : (b + 1) * CENTRES], flipped[:], identity[:])
 
-        def finish(b, candidates, flipped):
-            largest = work.tile([P, CENTRES], F32, name="largest")
-            nc.vector.tensor_reduce(largest[:], candidates, AXIS_X, ALU.max)
-            mean = work_psum.tile([P, CENTRES], F32, name="mean", tag="small")
-            nc.tensor.transpose(mean[:], flipped[:], identity[:])
-            pooled = work.tile([P, CENTRES], F32, name="pooled")
-            nc.vector.tensor_add(pooled[:], largest[:], mean[:])
-            result = work.tile([P, CENTRES], F32, name="result")
-            nc.scalar.activation(
-                result[:], pooled[:], ACT.Gelu, bias=bias[:, b : b + 1], scale=scale[:, b : b + 1]
-            )
-            nc.sync.dma_start(out[b * P : (b + 1) * P, :], result[:])
-
-        means = []
         for b in range(BLOCKS):
             for k in range(QUARTERS):
                 look_up(b, k)
                 if b == 0:
                     first_round(k)
-            means.append(flipped_mean(b))
+            take_mean(b)
 
-        finish(1, sums[1][:].rearrange("p (t r) -> p t r", r=GROUP), means[1])
-        finish(0, winners[:].rearrange("p (t r) -> p t r", r=GROUP // 2), means[0])
-        finish(2, sums[2][:].rearrange("p (t r) -> p t r", r=GROUP), means[2])
+        columns = held_psum.tile([P, BLOCKS, PARAMS], F32, name="columns")
+        for b in range(BLOCKS):
+            nc.tensor.matmul(
+                columns[:, b, :], rows[:, b * P : (b + 1) * P], identity[:PARAMS, :PARAMS], start=True, stop=True
+            )
+        running_mean, running_var, gain, shift = (columns[:, :, i] for i in range(PARAMS))
+
+        deviation = held.tile([P, BLOCKS], F32, name="deviation")
+        inverse = held.tile([P, BLOCKS], F32, name="inverse")
+        scale = held.tile([P, BLOCKS], F32, name="scale")
+        scaled_mean = held.tile([P, BLOCKS], F32, name="scaled_mean")
+        bias = held.tile([P, BLOCKS], F32, name="bias")
+        nc.scalar.activation(deviation[:], running_var, ACT.Sqrt, bias=EPS)
+        nc.vector.reciprocal(inverse[:], deviation[:])
+        nc.vector.tensor_mul(scale[:], gain, inverse[:])
+        nc.vector.tensor_mul(scaled_mean[:], running_mean, scale[:])
+        nc.vector.tensor_sub(bias[:], shift, scaled_mean[:])
+
+        maxima = held.tile([P, BLOCKS * CENTRES], F32, name="maxima")
+        for b in range(1, BLOCKS):
+            members = sums[b][:].rearrange("p (t r) -> p t r", r=GROUP)
+            nc.vector.tensor_reduce(maxima[:, b * CENTRES : (b + 1) * CENTRES], members, AXIS_X, ALU.max)
+        nc.vector.tensor_reduce(
+            maxima[:, :CENTRES], winners[:].rearrange("p (t r) -> p t r", r=GROUP // 2), AXIS_X, ALU.max
+        )
+        pooled = held.tile([P, BLOCKS * CENTRES], F32, name="pooled")
+        nc.vector.tensor_add(pooled[:], maxima[:], means[:])
+
+        for b in range(BLOCKS):
+            result = work.tile([P, CENTRES], F32, name="result")
+            nc.scalar.activation(
+                result[:],
+                pooled[:, b * CENTRES : (b + 1) * CENTRES],
+                ACT.Gelu,
+                bias=bias[:, b : b + 1],
+                scale=scale[:, b : b + 1],
+            )
+            nc.sync.dma_start(out[b * P : (b + 1) * P, :], result[:])

@@ -20,6 +20,9 @@ QUARTERS = ENTRIES // QUARTER
 PAIRS = QUARTER // 2
 CHUNKS = PAIRS // P
 FIRST_PIECE = 256
+EARLY = 2
+EARLY_CENTRES = EARLY * QUARTER // GROUP
+LATE_CENTRES = 64
 EPS = 1e-5
 PARAMS = 4
 FLOPS = 3 * CHANNELS * ENTRIES
@@ -70,7 +73,8 @@ def tile_block_kernel(tc, x, attn, bn_mean, bn_var, bn_g, bn_b, offs, out):
         make_identity(nc, identity[:])
 
         sums = [held.tile([P, ENTRIES], F32, name=f"summed{b}") for b in range(BLOCKS)]
-        winners = held.tile([P, ENTRIES // 2], F32, name="winners")
+        early_winners = held.tile([P, EARLY * PAIRS], F32, name="early_winners")
+        totals = held_psum.tile([P, BLOCKS * P], F32, name="totals")
         means = held_psum.tile([P, BLOCKS * CENTRES], F32, name="means")
 
         def look_up(b, k):
@@ -111,25 +115,51 @@ def tile_block_kernel(tc, x, attn, bn_mean, bn_var, bn_g, bn_b, offs, out):
                 nc.tensor.matmul(
                     better[:, chunk], second[:, chunk], identity[:], is_transpose=True, start=False, stop=True
                 )
-            nc.scalar.copy(winners[:, k * PAIRS : (k + 1) * PAIRS], better[:])
+            nc.scalar.copy(early_winners[:, k * PAIRS : (k + 1) * PAIRS], better[:])
 
-        def take_mean(b):
-            total = road_psum.tile([P, P], F32, name="total")
+        def late_round():
+            halves = sums[BLOCKS - 1][:, (CENTRES - LATE_CENTRES) * GROUP :].rearrange(
+                "p (t h r) -> p t h r", h=2, r=GROUP // 2
+            )
+            late_difference = held.tile([P, LATE_CENTRES, GROUP // 2], F32, name="late_difference")
+            late_excess = held.tile([P, LATE_CENTRES, GROUP // 2], F32, name="late_excess")
+            late_winners = held.tile([P, LATE_CENTRES, GROUP // 2], F32, name="late_winners")
+            parts = (slice(0, GROUP // 4), slice(GROUP // 4, GROUP // 2))
+            for part in parts:
+                nc.gpsimd.tensor_tensor(
+                    late_difference[:, :, part], halves[:, :, 0, part], halves[:, :, 1, part], ALU.subtract
+                )
+                nc.scalar.activation(late_excess[:, :, part], late_difference[:, :, part], ACT.Relu)
+            for part in parts:
+                nc.gpsimd.tensor_tensor(
+                    late_winners[:, :, part], halves[:, :, 1, part], late_excess[:, :, part], ALU.add
+                )
+            return late_winners
+
+        def add_members(b):
             by_member = sums[b][:].rearrange("p (t r) -> p r t", r=GROUP)
             for r in range(GROUP):
                 nc.tensor.matmul(
-                    total[:], by_member[:, r, :], identity[:], is_transpose=True, start=(r == 0), stop=(r == GROUP - 1)
+                    totals[:, b * P : (b + 1) * P],
+                    by_member[:, r, :],
+                    identity[:],
+                    is_transpose=True,
+                    start=(r == 0),
+                    stop=(r == GROUP - 1),
                 )
-            flipped = work.tile([P, P], F32, name="flipped")
-            nc.scalar.mul(flipped[:], total[:], 1.0 / GROUP)
-            nc.tensor.transpose(means[:, b * CENTRES : (b + 1) * CENTRES], flipped[:], identity[:])
 
         for b in range(BLOCKS):
             for k in range(QUARTERS):
                 look_up(b, k)
-                if b == 0:
+                if b == 0 and k < EARLY:
                     first_round(k)
-            take_mean(b)
+            add_members(b)
+        late_winners = late_round()
+
+        flipped = held.tile([P, BLOCKS * P], F32, name="flipped")
+        nc.scalar.mul(flipped[:], totals[:], 1.0 / GROUP)
+        for b in range(BLOCKS):
+            nc.tensor.transpose(means[:, b * CENTRES : (b + 1) * CENTRES], flipped[:, b * P : (b + 1) * P], identity[:])
 
         columns = held_psum.tile([P, BLOCKS, PARAMS], F32, name="columns")
         for b in range(BLOCKS):
@@ -150,12 +180,18 @@ def tile_block_kernel(tc, x, attn, bn_mean, bn_var, bn_g, bn_b, offs, out):
         nc.vector.tensor_sub(bias[:], shift, scaled_mean[:])
 
         maxima = held.tile([P, BLOCKS * CENTRES], F32, name="maxima")
-        for b in range(1, BLOCKS):
-            members = sums[b][:].rearrange("p (t r) -> p t r", r=GROUP)
-            nc.vector.tensor_reduce(maxima[:, b * CENTRES : (b + 1) * CENTRES], members, AXIS_X, ALU.max)
-        nc.vector.tensor_reduce(
-            maxima[:, :CENTRES], winners[:].rearrange("p (t r) -> p t r", r=GROUP // 2), AXIS_X, ALU.max
-        )
+
+        def take_max(b, first, end, candidates):
+            nc.vector.tensor_reduce(maxima[:, b * CENTRES + first : b * CENTRES + end], candidates, AXIS_X, ALU.max)
+
+        def members(b, first, end):
+            return sums[b][:, first * GROUP : end * GROUP].rearrange("p (t r) -> p t r", r=GROUP)
+
+        take_max(1, 0, CENTRES, members(1, 0, CENTRES))
+        take_max(0, EARLY_CENTRES, CENTRES, members(0, EARLY_CENTRES, CENTRES))
+        take_max(2, 0, CENTRES - LATE_CENTRES, members(2, 0, CENTRES - LATE_CENTRES))
+        take_max(0, 0, EARLY_CENTRES, early_winners[:].rearrange("p (t r) -> p t r", r=GROUP // 2))
+        take_max(2, CENTRES - LATE_CENTRES, CENTRES, late_winners[:])
         pooled = held.tile([P, BLOCKS * CENTRES], F32, name="pooled")
         nc.vector.tensor_add(pooled[:], maxima[:], means[:])
 

@@ -187,21 +187,26 @@ def tile_block_kernel(tc, x, attn, bn_mean, bn_var, bn_g, bn_b, offs, out):
         def members(b, first, end):
             return sums[b][:, first * GROUP : end * GROUP].rearrange("p (t r) -> p t r", r=GROUP)
 
+        pooled = held.tile([P, BLOCKS * CENTRES], F32, name="pooled")
+
+        def finish(first_block, end_block):
+            columns_of = slice(first_block * CENTRES, end_block * CENTRES)
+            nc.vector.tensor_add(pooled[:, columns_of], maxima[:, columns_of], means[:, columns_of])
+            for b in range(first_block, end_block):
+                result = work.tile([P, CENTRES], F32, name="result")
+                nc.scalar.activation(
+                    result[:],
+                    pooled[:, b * CENTRES : (b + 1) * CENTRES],
+                    ACT.Gelu,
+                    bias=bias[:, b : b + 1],
+                    scale=scale[:, b : b + 1],
+                )
+                nc.sync.dma_start(out[b * P : (b + 1) * P, :], result[:])
+
         take_max(1, 0, CENTRES, members(1, 0, CENTRES))
         take_max(0, EARLY_CENTRES, CENTRES, members(0, EARLY_CENTRES, CENTRES))
-        take_max(2, 0, CENTRES - LATE_CENTRES, members(2, 0, CENTRES - LATE_CENTRES))
         take_max(0, 0, EARLY_CENTRES, early_winners[:].rearrange("p (t r) -> p t r", r=GROUP // 2))
+        take_max(2, 0, CENTRES - LATE_CENTRES, members(2, 0, CENTRES - LATE_CENTRES))
+        finish(0, BLOCKS - 1)
         take_max(2, CENTRES - LATE_CENTRES, CENTRES, late_winners[:])
-        pooled = held.tile([P, BLOCKS * CENTRES], F32, name="pooled")
-        nc.vector.tensor_add(pooled[:], maxima[:], means[:])
-
-        for b in range(BLOCKS):
-            result = work.tile([P, CENTRES], F32, name="result")
-            nc.scalar.activation(
-                result[:],
-                pooled[:, b * CENTRES : (b + 1) * CENTRES],
-                ACT.Gelu,
-                bias=bias[:, b : b + 1],
-                scale=scale[:, b : b + 1],
-            )
-            nc.sync.dma_start(out[b * P : (b + 1) * P, :], result[:])
+        finish(BLOCKS - 1, BLOCKS)

@@ -157,9 +157,13 @@ def tile_block_kernel(tc, x, attn, bn_mean, bn_var, bn_g, bn_b, offs, out):
         late_winners = late_round()
 
         flipped = held.tile([P, BLOCKS * P], F32, name="flipped")
-        nc.scalar.mul(flipped[:], totals[:], 1.0 / GROUP)
-        for b in range(BLOCKS):
-            nc.tensor.transpose(means[:, b * CENTRES : (b + 1) * CENTRES], flipped[:, b * P : (b + 1) * P], identity[:])
+        for first_block, end_block in ((0, BLOCKS - 1), (BLOCKS - 1, BLOCKS)):
+            columns_of = slice(first_block * P, end_block * P)
+            nc.scalar.mul(flipped[:, columns_of], totals[:, columns_of], 1.0 / GROUP)
+            for b in range(first_block, end_block):
+                nc.tensor.transpose(
+                    means[:, b * CENTRES : (b + 1) * CENTRES], flipped[:, b * P : (b + 1) * P], identity[:]
+                )
 
         columns = held_psum.tile([P, BLOCKS, PARAMS], F32, name="columns")
         for b in range(BLOCKS):

import concourse.mybir as mybir
from concourse.masks import make_identity

F32 = mybir.dt.float32
U16 = mybir.dt.uint16
ALU = mybir.AluOpType
ACT = mybir.ActivationFunctionType
AXIS_X = mybir.AxisListType.X

P = 128
CHANNELS = 384
BLOCKS = CHANNELS // P
STORE = 2048
ENTRIES = 4096
PER_COLUMN = 16
GROUP = 32
CENTRES = ENTRIES // GROUP
QUARTER = 1024
QUARTERS = ENTRIES // QUARTER
PAIRS = QUARTER // 2
CHUNKS = PAIRS // P
FIRST_PIECE = 256
EARLY = 2
EARLY_CENTRES = EARLY * QUARTER // GROUP
LATE_CENTRES = 64
EPS = 1e-5
PARAMS = 4
FLOPS = 3 * CHANNELS * ENTRIES


def pieces_of(b, k):
    first, end = k * QUARTER, (k + 1) * QUARTER
    if b == 0 and k == 0:
        return [(first, FIRST_PIECE), (FIRST_PIECE, end)]
    return [(first, end)]


def tile_block_kernel(tc, x, attn, bn_mean, bn_var, bn_g, bn_b, offs, out):
    nc = tc.nc
    with (
        tc.tile_pool(name="held", bufs=1) as held,
        tc.psum_pool(name="held_psum", bufs=1) as held_psum,
        tc.tile_pool(name="road", bufs=3) as road,
        tc.psum_pool(name="road_psum", bufs=2) as road_psum,
        tc.psum_pool(name="turned_psum", bufs=1) as turned_psum,
        tc.tile_pool(name="work", bufs=BLOCKS) as work,
    ):
        offsets = held.tile([P, ENTRIES // PER_COLUMN], U16, name="offsets")
        nc.sync.dma_start(offsets[:], offs)

        stores = []
        branches = []
        loads = []
        for b in range(BLOCKS):
            channels = slice(b * P, (b + 1) * P)
            store = held.tile([P, STORE], F32, name=f"store{b}")
            loads.append((store[:], x[channels, :]))
            branch = held.tile([P, ENTRIES], F32, name=f"branch{b}")
            for k in range(QUARTERS):
                for first, end in pieces_of(b, k):
                    loads.append((branch[:, first:end], attn[channels, first:end]))
            stores.append(store)
            branches.append(branch)
        rows = held.tile([PARAMS, CHANNELS], F32, name="rows")
        for n, (part, source) in enumerate(loads):
            queue = nc.sync if n % 2 == 0 else nc.scalar
            queue.dma_start(part, source)
            if n == 0:
                for i, vector in enumerate((bn_mean, bn_var, bn_g, bn_b)):
                    nc.sync.dma_start(rows[i : i + 1, :], vector.rearrange("c o -> o c"))

        identity = held.tile([P, P], F32, name="identity")
        make_identity(nc, identity[:])

        sums = [held.tile([P, ENTRIES], F32, name=f"summed{b}") for b in range(BLOCKS)]
        early_winners = held.tile([P, EARLY * PAIRS], F32, name="early_winners")
        totals = held_psum.tile([P, BLOCKS * P], F32, name="totals")
        means = held_psum.tile([P, BLOCKS * CENTRES], F32, name="means")

        def look_up(b, k):
            for first, end in pieces_of(b, k):
                entries = slice(first, end)
                piece = offsets[:, first // PER_COLUMN : end // PER_COLUMN]
                nc.vector.tensor_tensor(
                    sums[b][:, entries], stores[b][:].indirect(piece), branches[b][:, entries], ALU.add
                )

        def first_round(k):
            pairs = sums[0][:, k * QUARTER : (k + 1) * QUARTER].rearrange("p (n two) -> p two n", two=2)
            negative = road.tile([P, PAIRS], F32, name="negative")
            nc.scalar.mul(negative[:], pairs[:, 1, :], -1.0)
            difference = road_psum.tile([P, PAIRS], F32, name="difference")
            for q in range(CHUNKS):
                chunk = slice(q * P, (q + 1) * P)
                nc.tensor.matmul(
                    difference[:, chunk], pairs[:, 0, chunk], identity[:], is_transpose=True, start=True, stop=False
                )
                nc.tensor.matmul(
                    difference[:, chunk], negative[:, chunk], identity[:], is_transpose=True, start=False, stop=True
                )
            turned = turned_psum.tile([P, PAIRS], F32, name="turned")
            for q in range(CHUNKS):
                chunk = slice(q * P, (q + 1) * P)
                nc.tensor.transpose(turned[:, chunk], negative[:, chunk], identity[:])
            excess = road.tile([P, PAIRS], F32, name="excess")
            nc.scalar.activation(excess[:], difference[:], ACT.Relu)
            second = road.tile([P, PAIRS], F32, name="second")
            nc.scalar.mul(second[:], turned[:], -1.0)
            better = turned_psum.tile([P, PAIRS], F32, name="better")
            for q in range(CHUNKS):
                chunk = slice(q * P, (q + 1) * P)
                nc.tensor.matmul(
                    better[:, chunk], excess[:, chunk], identity[:], is_transpose=True, start=True, stop=False
                )
                nc.tensor.matmul(
                    better[:, chunk], second[:, chunk], identity[:], is_transpose=True, start=False, stop=True
                )
            nc.scalar.copy(early_winners[:, k * PAIRS : (k + 1) * PAIRS], better[:])

        def late_round():
            halves = sums[BLOCKS - 1][:, (CENTRES - LATE_CENTRES) * GROUP :].rearrange(
                "p (t h r) -> p t h r", h=2, r=GROUP // 2
            )
            late_difference = held.tile([P, LATE_CENTRES, GROUP // 2], F32, name="late_difference")
            late_excess = held.tile([P, LATE_CENTRES, GROUP // 2], F32, name="late_excess")
            late_winners = held.tile([P, LATE_CENTRES, GROUP // 2], F32, name="late_winners")
            parts = (slice(0, GROUP // 4), slice(GROUP // 4, GROUP // 2))
            for part in parts:
                nc.gpsimd.tensor_tensor(
                    late_difference[:, :, part], halves[:, :, 0, part], halves[:, :, 1, part], ALU.subtract
                )
                nc.scalar.activation(late_excess[:, :, part], late_difference[:, :, part], ACT.Relu)
            for part in parts:
                nc.gpsimd.tensor_tensor(
                    late_winners[:, :, part], halves[:, :, 1, part], late_excess[:, :, part], ALU.add
                )
            return late_winners

        def add_members(b):
            by_member = sums[b][:].rearrange("p (t r) -> p r t", r=GROUP)
            for r in range(GROUP):
                nc.tensor.matmul(
                    totals[:, b * P : (b + 1) * P],
                    by_member[:, r, :],
                    identity[:],
                    is_transpose=True,
                    start=(r == 0),
                    stop=(r == GROUP - 1),
                )

        for b in range(BLOCKS):
            for k in range(QUARTERS):
                look_up(b, k)
                if b == 0 and k < EARLY:
                    first_round(k)
            add_members(b)
        late_winners = late_round()

        flipped = held.tile([P, BLOCKS * P], F32, name="flipped")
        for first_block, end_block in ((0, BLOCKS - 1), (BLOCKS - 1, BLOCKS)):
            columns_of = slice(first_block * P, end_block * P)
            nc.scalar.mul(flipped[:, columns_of], totals[:, columns_of], 1.0 / GROUP)
            for b in range(first_block, end_block):
                nc.tensor.transpose(
                    means[:, b * CENTRES : (b + 1) * CENTRES], flipped[:, b * P : (b + 1) * P], identity[:]
                )

        columns = held_psum.tile([P, BLOCKS, PARAMS], F32, name="columns")
        for b in range(BLOCKS):
            nc.tensor.matmul(
                columns[:, b, :], rows[:, b * P : (b + 1) * P], identity[:PARAMS, :PARAMS], start=True, stop=True
            )
        running_mean, running_var, gain, shift = (columns[:, :, i] for i in range(PARAMS))

        deviation = held.tile([P, BLOCKS], F32, name="deviation")
        inverse = held.tile([P, BLOCKS], F32, name="inverse")
        scale = held.tile([P, BLOCKS], F32, name="scale")
        scaled_mean = held.tile([P, BLOCKS], F32, name="scaled_mean")
        bias = held.tile([P, BLOCKS], F32, name="bias")
        nc.scalar.activation(deviation[:], running_var, ACT.Sqrt, bias=EPS)
        nc.vector.reciprocal(inverse[:], deviation[:])
        nc.vector.tensor_mul(scale[:], gain, inverse[:])
        nc.vector.tensor_mul(scaled_mean[:], running_mean, scale[:])
        nc.vector.tensor_sub(bias[:], shift, scaled_mean[:])

        maxima = held.tile([P, BLOCKS * CENTRES], F32, name="maxima")

        def take_max(b, first, end, candidates):
            nc.vector.tensor_reduce(maxima[:, b * CENTRES + first : b * CENTRES + end], candidates, AXIS_X, ALU.max)

        def members(b, first, end):
            return sums[b][:, first * GROUP : end * GROUP].rearrange("p (t r) -> p t r", r=GROUP)

        pooled = held.tile([P, BLOCKS * CENTRES], F32, name="pooled")

        def finish(first_block, end_block):
            columns_of = slice(first_block * CENTRES, end_block * CENTRES)
            nc.vector.tensor_add(pooled[:, columns_of], maxima[:, columns_of], means[:, columns_of])
            for b in range(first_block, end_block):
                result = work.tile([P, CENTRES], F32, name="result")
                nc.scalar.activation(
                    result[:],
                    pooled[:, b * CENTRES : (b + 1) * CENTRES],
                    ACT.Gelu,
                    bias=bias[:, b : b + 1],
                    scale=scale[:, b : b + 1],
                )
                nc.sync.dma_start(out[b * P : (b + 1) * P, :], result[:])

        take_max(1, 0, CENTRES, members(1, 0, CENTRES))
        take_max(0, EARLY_CENTRES, CENTRES, members(0, EARLY_CENTRES, CENTRES))
        take_max(0, 0, EARLY_CENTRES, early_winners[:].rearrange("p (t r) -> p t r", r=GROUP // 2))
        take_max(2, 0, CENTRES - LATE_CENTRES, members(2, 0, CENTRES - LATE_CENTRES))
        finish(0, BLOCKS - 1)
        take_max(2, CENTRES - LATE_CENTRES, CENTRES, late_winners[:])
        finish(BLOCKS - 1, BLOCKS)
